import numpy as np
import ml_dtypes


def mxq(x, axis, fmt="e4m3"):
    dtype, down = {"e4m3": (ml_dtypes.float8_e4m3fn, 7), "e5m2": (ml_dtypes.float8_e5m2, 14)}[fmt]
    v = np.moveaxis(np.asarray(x, np.float32).astype(ml_dtypes.bfloat16).astype(np.float64), axis, -1)
    blocks = v.reshape(v.shape[:-1] + (-1, 32))
    amax = np.abs(blocks).max(-1, keepdims=True)
    byte = np.maximum(np.where(amax > 0, np.frexp(amax)[1] - 1 + 127, 0) - down, 1)
    scale = np.exp2(byte - 127.0)
    codes = (blocks / scale).astype(np.float32).astype(dtype).astype(np.float64)
    return np.moveaxis((codes * scale).reshape(v.shape), -1, axis)


WIDE = False


def mx_kscale(k):
    if not WIDE:
        return np.ones(k)
    levels = np.array([10, -10, 5, -5, 0])
    if k % 512:
        return np.exp2(np.random.permutation(np.resize(levels, k // 32))).repeat(32)
    a = np.empty((k // 512, 16))
    for p in range(k // 512):
        a[p, :8] = np.random.permutation(np.resize(levels, 8))
        for g in range(8):
            far = levels[np.abs(levels - a[p, g]) >= 10]
            a[p, g + 8] = far[np.random.randint(len(far))]
    return np.exp2(a.ravel()).repeat(32)


BF16 = ml_dtypes.bfloat16


def bf(x):
    return np.asarray(x, np.float32).astype(BF16)


def f64(x):
    return np.asarray(x).astype(np.float64)


B, T, DX, DY, F = 128, 5, 8192, 512, 3
MIN_CONTEXT = 1
G = 1.5 / DY ** 0.25


def setup_inputs():
    s, t = mx_kscale(DX), mx_kscale(DY)
    return {"embeddings": bf(np.random.standard_normal((B, T, DX)) * s),
            "contexts": bf(np.random.standard_normal((B, T, DY)) * G / t),
            "W": bf(np.random.standard_normal((F, DY, DX)) * G / np.sqrt(DX) * t[:, None] / s)}


def reference(embeddings, contexts, W):
    eq = mxq(f64(embeddings)[:, MIN_CONTEXT:T], 2, "e4m3")
    cq = mxq(f64(contexts)[:, MIN_CONTEXT - 1:T - 1], 2, "e4m3")
    wq = mxq(f64(W), 2, "e4m3")
    losses = []
    for step in range(F):
        S = T - step - MIN_CONTEXT
        xw = eq[:, step:] @ wq[step].T
        scores = mxq(xw, 2, "e4m3").transpose(1, 0, 2) @ cq[:, :S].transpose(1, 2, 0)
        pos = np.diagonal(scores, axis1=1, axis2=2)
        m = scores.max(2, keepdims=True)
        lse = np.log(np.exp(scores - m).sum(2)) + m[:, :, 0] - np.log(B * S)
        losses.append((lse - pos).T.reshape(-1))
    return np.concatenate(losses)

@@ -1,0 +1,312 @@
+from contextlib import ExitStack
+
+import concourse.mybir as mybir
+from concourse.masks import make_identity
+
+F32 = mybir.dt.float32
+BF16 = mybir.dt.bfloat16
+U32 = mybir.dt.uint32
+U8 = mybir.dt.uint8
+FP8X4 = mybir.dt.float8_e4m3fn_x4
+ACT = mybir.ActivationFunctionType
+ALU = mybir.AluOpType
+AXIS = mybir.AxisListType
+
+P = 128
+DX = 8192
+DY = 512
+STEPS = 3
+TIMES = 4
+PACK = 4
+K_PASS = P * PACK
+PASSES = DX // K_PASS
+BLOCKS = 4
+ROWS = BLOCKS * P
+LOAD_PASSES = 2
+LOAD_D = LOAD_PASSES * K_PASS
+PASS_WORDS = K_PASS // 2
+LAG = 2
+GATHER = 8
+
+FLOPS = 2 * (4 + 3 + 2) * P * DY * DX + 2 * (4 + 3 + 2) * P * P * DY
+BYTES = 2 * (P * TIMES * DX + P * TIMES * DY + STEPS * DY * DX) + 4 * (4 + 3 + 2) * P
+
+
+def tile_infonceloss_pa_k_kernel(tc, embeddings, contexts, W, out):
+    nc = tc.nc
+    with ExitStack() as ctx:
+        consts = ctx.enter_context(tc.tile_pool(name="consts", bufs=1))
+        keep = ctx.enter_context(tc.tile_pool(name="keep", bufs=1))
+        x_loads = ctx.enter_context(tc.tile_pool(name="x_loads", bufs=3))
+        w_loads = ctx.enter_context(tc.tile_pool(name="w_loads", bufs=8))
+        stage = ctx.enter_context(tc.tile_pool(name="stage", bufs=4))
+        w_mx = ctx.enter_context(tc.tile_pool(name="w_mx", bufs=2 * (LAG + 2)))
+        second = ctx.enter_context(tc.tile_pool(name="second", bufs=2))
+        xw_rows = ctx.enter_context(tc.tile_pool(name="xw_rows", bufs=TIMES))
+        e_stage = ctx.enter_context(tc.tile_pool(name="e_stage", bufs=2))
+        sums_psum = ctx.enter_context(tc.psum_pool(name="sums_psum", bufs=1))
+        work_psum = ctx.enter_context(tc.psum_pool(name="work_psum", bufs=4))
+        ctx.enter_context(tc.manual_schedule())
+
+        ident_f32 = consts.tile([P, P], F32)
+        make_identity(nc, ident_f32[:])
+        ident_bf16 = consts.tile([P, P], BF16)
+        make_identity(nc, ident_bf16[:])
+        group = consts.tile([P, P], F32)
+        nc.vector.memset(group[:], 0.0)
+        nc.vector.tensor_reduce(
+            out=group[:, 0 : P // GATHER],
+            in_=ident_f32[:].rearrange("p (h l) -> p h l", l=GATHER),
+            axis=AXIS.X,
+            op=ALU.add,
+        )
+        place = consts.tile([P, GATHER], F32)
+        nc.vector.tensor_reduce(
+            out=place[:], in_=ident_f32[:].rearrange("p (h l) -> p l h", l=GATHER), axis=AXIS.X, op=ALU.add
+        )
+        warm = consts.tile([P, 1], F32)
+        nc.scalar.activation(out=warm[:], in_=place[:, 0:1], func=ACT.Exp)
+
+        def load_rows(pool, rows_view, load):
+            raw = pool.tile([P, BLOCKS * LOAD_D], BF16, tag="raw")
+            nc.sync.dma_start(
+                out=raw[:].rearrange("p (r d) -> p r d", r=BLOCKS),
+                in_=rows_view[:, :, load * LOAD_D : (load + 1) * LOAD_D],
+            )
+            return raw
+
+        def turn_pass(raw, g, vector_copies_last):
+            words = raw[:].bitcast(F32)
+            grouped = stage.tile([P, ROWS * PACK], BF16, tag="grouped", align_bytes=64)
+            grouped_words = grouped[:].bitcast(F32).rearrange("p (c u) -> p c u", u=2)
+            for half in range(2):
+                bank = work_psum.tile([P, 2, 2 * P], F32, tag="work")
+                for blk in range(2):
+                    for u in range(2):
+                        first = ((2 * half + blk) * LOAD_PASSES + g % LOAD_PASSES) * PASS_WORDS
+                        nc.tensor.transpose(
+                            bank[:, u, blk * P : (blk + 1) * P],
+                            words[:, first + u : first + PASS_WORDS : 2],
+                            ident_f32[:],
+                        )
+                side_by_side = grouped_words[:, half * 2 * P : (half + 1) * 2 * P, :]
+                if half == 1 and vector_copies_last:
+                    nc.vector.tensor_copy(out=side_by_side, in_=bank[:].rearrange("p u c -> p c u"))
+                else:
+                    nc.scalar.copy(out=side_by_side, in_=bank[:].rearrange("p u c -> p c u"))
+            return grouped
+
+        def quantise(grouped, codes, scales):
+            nc.vector.quantize_mx(out=codes.bitcast(FP8X4), scales=scales, in_=grouped[:])
+
+        def turn_rows(rows_list, bank, on_scalar):
+            n = len(rows_list)
+            turned = sums_psum.tile([P, n, PACK, P], BF16, tag=bank)
+            for i in range(n):
+                for t in range(PACK):
+                    nc.tensor.transpose(turned[:, i, t, :], rows_list[i][:, t, :], ident_bf16[:])
+            grouped = e_stage.tile([P, n * P * PACK], BF16, tag="grouped_e", align_bytes=64)
+            side_by_side = grouped[:].rearrange("p (i r t) -> p i r t", i=n, t=PACK)
+            if on_scalar:
+                nc.scalar.copy(out=side_by_side, in_=turned[:].rearrange("p i t r -> p i r t"))
+            else:
+                nc.vector.tensor_copy(out=side_by_side, in_=turned[:].rearrange("p i t r -> p i r t"))
+            return grouped
+
+        def own_bank(k):
+            return "sums%d" % (TIMES - 1 - k)
+
+        def pairs(k):
+            return (TIMES - k + 1) // 2
+
+        xw = {}
+        xw_codes = {}
+        xw_scales = {}
+        scores = {}
+        top = {}
+        minus_top = {}
+        top_less_positive = {}
+        exp_sums = {}
+        log_mean = {}
+        placed = {}
+        gathered = {}
+
+        def round_xw(k):
+            xw_codes[k] = second.tile([P, TIMES * P], U32, tag="xw_codes", align_bytes=64, name="xw_codes_%d" % k)
+            xw_scales[k] = second.tile([P, TIMES * P], U8, tag="xw_scales", align_bytes=64, name="xw_scales_%d" % k)
+            for s in range(TIMES - k):
+                xw[(k, s)] = xw_rows.tile([P, DY], BF16, tag="xw", name="xw_%d_%d" % (k, s))
+                if s % 2 == 0:
+                    nc.scalar.copy(out=xw[(k, s)][:], in_=sums[(k, s)][:])
+                else:
+                    nc.vector.tensor_copy(out=xw[(k, s)][:], in_=sums[(k, s)][:])
+
+        def turn_xw(k, pair):
+            times = range(2 * pair, min(2 * pair + 2, TIMES - k))
+            cols = slice(times[0] * P, (times[-1] + 1) * P)
+            rows = [xw[(k, s)][:].rearrange("b (t p) -> b t p", t=PACK) for s in times]
+            grouped = turn_rows(rows, own_bank(k), pair % 2 == 1)
+            return (grouped, xw_codes[k][:, cols], xw_scales[k][:, cols])
+
+        def score(k):
+            n_s = TIMES - k
+            scores[k] = sums_psum.tile([P, n_s, P], F32, tag=own_bank(k), name="scores_%d" % k)
+            for s in range(n_s):
+                cols = slice(s * P, (s + 1) * P)
+                nc.tensor.matmul_mx(
+                    out=scores[k][:, s, :],
+                    lhsT=xw_codes[k][:, cols].bitcast(FP8X4),
+                    lhsT_scale=xw_scales[k][:, cols],
+                    rhs=c_codes[:, cols].bitcast(FP8X4),
+                    rhs_scale=c_scales[:, cols],
+                    start=True,
+                    stop=True,
+                )
+            top[k] = second.tile([P, n_s], F32, tag="top", name="top_%d" % k)
+            nc.vector.tensor_reduce(out=top[k][:], in_=scores[k][:], axis=AXIS.X, op=ALU.max)
+            minus_top[k] = second.tile([P, n_s], F32, tag="minus_top", name="minus_top_%d" % k)
+            nc.vector.tensor_scalar_mul(out=minus_top[k][:], in0=top[k][:], scalar1=-1.0)
+
+        def diagonal(k):
+            n_s = TIMES - k
+            on_diagonal = second.tile([P, n_s, P], F32, tag="on_diagonal")
+            nc.vector.tensor_tensor(
+                out=on_diagonal[:],
+                in0=scores[k][:],
+                in1=ident_f32[:].unsqueeze(1).to_broadcast([P, n_s, P]),
+                op=ALU.mult,
+            )
+            positive = second.tile([P, n_s], F32, tag="positive")
+            nc.vector.tensor_reduce(out=positive[:], in_=on_diagonal[:], axis=AXIS.X, op=ALU.add)
+            top_less_positive[k] = second.tile([P, n_s], F32, tag="top_less_positive", name="tlp_%d" % k)
+            nc.vector.tensor_sub(out=top_less_positive[k][:], in0=top[k][:], in1=positive[:])
+
+        def exponentials(k):
+            n_s = TIMES - k
+            exps = second.tile([P, n_s, P], F32, tag="exps")
+            exp_sums[k] = second.tile([P, n_s], F32, tag="exp_sums", name="exp_sums_%d" % k)
+            for s in range(n_s):
+                nc.scalar.activation(
+                    out=exps[:, s, :],
+                    in_=scores[k][:, s, :],
+                    func=ACT.Exp,
+                    bias=minus_top[k][:, s : s + 1],
+                    scale=1.0,
+                    accum_out=exp_sums[k][:, s : s + 1],
+                )
+
+        def logarithm(k):
+            n_s = TIMES - k
+            log_mean[k] = second.tile([P, n_s], F32, tag="log_mean", name="log_mean_%d" % k)
+            nc.scalar.activation(out=log_mean[k][:], in_=exp_sums[k][:], func=ACT.Ln, scale=1.0 / (P * n_s))
+
+        def place_loss(k):
+            n_s = TIMES - k
+            loss = second.tile([P, n_s], F32, tag="loss")
+            nc.vector.tensor_add(out=loss[:], in0=log_mean[k][:], in1=top_less_positive[k][:])
+            placed[k] = second.tile([P, GATHER, n_s], F32, tag="placed", name="placed_%d" % k)
+            nc.vector.tensor_tensor(
+                out=placed[k][:],
+                in0=place[:].unsqueeze(2).to_broadcast([P, GATHER, n_s]),
+                in1=loss[:].unsqueeze(1).to_broadcast([P, GATHER, n_s]),
+                op=ALU.mult,
+            )
+
+        def gather(k):
+            gathered[k] = sums_psum.tile([P, GATHER * (TIMES - k)], F32, tag=own_bank(k), name="gathered_%d" % k)
+            nc.tensor.matmul(
+                out=gathered[k][:], lhsT=group[:], rhs=placed[k][:].rearrange("p l s -> p (l s)"), start=True, stop=True
+            )
+
+        def store(k):
+            groups = P // GATHER
+            n = GATHER * (TIMES - k)
+            runs = second.tile([groups, n], F32, tag="runs")
+            nc.scalar.copy(out=runs[:], in_=gathered[k][0:groups, :])
+            first = sum(P * (TIMES - j) for j in range(k))
+            nc.scalar.dma_start(out=out[first : first + groups * n].rearrange("(h n) -> h n", h=groups), in_=runs[:])
+
+        c_raw = keep.tile([P, TIMES * DY], BF16)
+        nc.sync.dma_start(out=c_raw[:].rearrange("p (t e) -> p t e", t=TIMES), in_=contexts[:, 0:TIMES, :])
+        c_codes = keep.tile([P, TIMES * P], U32, align_bytes=64)
+        c_scales = keep.tile([P, TIMES * P], U8, align_bytes=64)
+        c_rows = [c_raw[:, s * DY : (s + 1) * DY].rearrange("b (p t) -> b t p", t=PACK) for s in range(TIMES)]
+        c_turned = [turn_rows(c_rows[2 * pair : 2 * pair + 2], "sums%d" % pair, pair % 2 == 1) for pair in range(2)]
+        for pair in range(2):
+            cols = slice(2 * pair * P, 2 * (pair + 1) * P)
+            quantise(c_turned[pair], c_codes[:, cols], c_scales[:, cols])
+
+        x_view = embeddings[:, 1 : 1 + TIMES, :]
+        x_codes = keep.tile([P, PASSES * ROWS], U32, align_bytes=64)
+        x_scales = keep.tile([P, PASSES * ROWS], U8, align_bytes=64)
+        sums = {}
+
+        def multiply(k, g, w_codes, w_scales):
+            for s in range(TIMES - k):
+                if g == 0:
+                    sums[(k, s)] = sums_psum.tile([P, DY], F32, tag="sums%d" % s, name="sums_%d_%d" % (k, s))
+                cols = slice(g * ROWS + (k + s) * P, g * ROWS + (k + s + 1) * P)
+                nc.tensor.matmul_mx(
+                    out=sums[(k, s)][:],
+                    lhsT=x_codes[:, cols].bitcast(FP8X4),
+                    lhsT_scale=x_scales[:, cols],
+                    rhs=w_codes[:].bitcast(FP8X4),
+                    rhs_scale=w_scales[:],
+                    start=(g == 0),
+                    stop=(g == PASSES - 1),
+                )
+
+        plan = []
+        for k in range(STEPS):
+            w_passes = 1 if k == 0 else 2
+            for first in range(0, PASSES, w_passes):
+                plan.append((k, range(first, first + w_passes)))
+
+        quantised = {}
+        closed_in = {}
+        for rnd in range(len(plan) + LAG + TIMES + 7):
+            turned = []
+            quantised[rnd] = []
+            if rnd < len(plan):
+                k, w_passes = plan[rnd]
+                if k == 0:
+                    g = rnd
+                    if g % LOAD_PASSES == 0:
+                        x_raw = load_rows(x_loads, x_view, g // LOAD_PASSES)
+                    cols = slice(g * ROWS, (g + 1) * ROWS)
+                    turned.append((turn_pass(x_raw, g, False), x_codes[:, cols], x_scales[:, cols]))
+                for g in w_passes:
+                    if g % LOAD_PASSES == 0:
+                        w_view = W[k].rearrange("(p r) d -> p r d", r=BLOCKS)
+                        w_raw = load_rows(w_loads, w_view, g // LOAD_PASSES)
+                    w_codes = w_mx.tile([P, ROWS], U32, tag="w_codes", align_bytes=64)
+                    w_scales = w_mx.tile([P, ROWS], U8, tag="w_scales", align_bytes=64)
+                    turned.append((turn_pass(w_raw, g, len(turned) == 1), w_codes[:], w_scales[:]))
+                    quantised[rnd].append((k, g, w_codes, w_scales))
+            for done in sorted(closed_in):
+                pair = rnd - closed_in[done] - 1
+                if 0 <= pair < pairs(done):
+                    turned.append(turn_xw(done, pair))
+            for grouped, codes, scales in turned:
+                quantise(grouped, codes, scales)
+            for k, g, w_codes, w_scales in quantised.get(rnd - LAG, []):
+                multiply(k, g, w_codes, w_scales)
+                if g == PASSES - 1:
+                    closed_in[k] = rnd
+            for done in sorted(closed_in):
+                if rnd == closed_in[done]:
+                    round_xw(done)
+                since_turned = rnd - closed_in[done] - pairs(done)
+                if since_turned == 1:
+                    score(done)
+                if since_turned == 2:
+                    exponentials(done)
+                if since_turned == 3:
+                    logarithm(done)
+                    diagonal(done)
+                if since_turned == 4:
+                    place_loss(done)
+                if since_turned == 5:
+                    gather(done)
+                if since_turned == 6:
+                    store(done)

@@ -25,6 +25,7 @@ ROWS = BLOCKS * P
 LOAD_PASSES = 2
 LOAD_D = LOAD_PASSES * K_PASS
 PASS_WORDS = K_PASS // 2
+HALF_BLOCK = 8
 LAG = 2
 GATHER = 8
 
@@ -38,8 +39,9 @@ def tile_infonceloss_pa_k_kernel(tc, embeddings, contexts, W, out):
         consts = ctx.enter_context(tc.tile_pool(name="consts", bufs=1))
         keep = ctx.enter_context(tc.tile_pool(name="keep", bufs=1))
         x_loads = ctx.enter_context(tc.tile_pool(name="x_loads", bufs=3))
-        w_loads = ctx.enter_context(tc.tile_pool(name="w_loads", bufs=8))
-        stage = ctx.enter_context(tc.tile_pool(name="stage", bufs=4))
+        w_loads = ctx.enter_context(tc.tile_pool(name="w_loads", bufs=7))
+        sorted_loads = ctx.enter_context(tc.tile_pool(name="sorted_loads", bufs=2))
+        stage = ctx.enter_context(tc.tile_pool(name="stage", bufs=6))
         w_mx = ctx.enter_context(tc.tile_pool(name="w_mx", bufs=2 * (LAG + 2)))
         second = ctx.enter_context(tc.tile_pool(name="second", bufs=2))
         xw_rows = ctx.enter_context(tc.tile_pool(name="xw_rows", bufs=TIMES))
@@ -75,25 +77,28 @@ def tile_infonceloss_pa_k_kernel(tc, embeddings, contexts, W, out):
             )
             return raw
 
-        def turn_pass(raw, g, vector_copies_last):
-            words = raw[:].bitcast(F32)
+        def sort_halves(raw, tag):
+            halves = sorted_loads.tile([P, BLOCKS * LOAD_D], BF16, tag=tag)
+            nc.vector.tensor_copy(
+                out=halves[:].rearrange("p (rg u q i) -> p rg u q i", rg=BLOCKS * LOAD_PASSES, u=2, i=2 * HALF_BLOCK),
+                in_=raw[:].rearrange("p (rg q u i) -> p rg u q i", rg=BLOCKS * LOAD_PASSES, u=2, i=2 * HALF_BLOCK),
+            )
+            return halves
+
+        def turn_pass(halves, g):
+            words = halves[:].bitcast(F32)
             grouped = stage.tile([P, ROWS * PACK], BF16, tag="grouped", align_bytes=64)
             grouped_words = grouped[:].bitcast(F32).rearrange("p (c u) -> p c u", u=2)
             for half in range(2):
                 bank = work_psum.tile([P, 2, 2 * P], F32, tag="work")
                 for blk in range(2):
                     for u in range(2):
-                        first = ((2 * half + blk) * LOAD_PASSES + g % LOAD_PASSES) * PASS_WORDS
+                        first = ((2 * half + blk) * LOAD_PASSES + g % LOAD_PASSES) * PASS_WORDS + u * P
                         nc.tensor.transpose(
-                            bank[:, u, blk * P : (blk + 1) * P],
-                            words[:, first + u : first + PASS_WORDS : 2],
-                            ident_f32[:],
+                            bank[:, u, blk * P : (blk + 1) * P], words[:, first : first + P], ident_f32[:]
                         )
                 side_by_side = grouped_words[:, half * 2 * P : (half + 1) * 2 * P, :]
-                if half == 1 and vector_copies_last:
-                    nc.vector.tensor_copy(out=side_by_side, in_=bank[:].rearrange("p u c -> p c u"))
-                else:
-                    nc.scalar.copy(out=side_by_side, in_=bank[:].rearrange("p u c -> p c u"))
+                nc.scalar.copy(out=side_by_side, in_=bank[:].rearrange("p u c -> p c u"))
             return grouped
 
         def quantise(grouped, codes, scales):
@@ -262,6 +267,27 @@ def tile_infonceloss_pa_k_kernel(tc, embeddings, contexts, W, out):
             for first in range(0, PASSES, w_passes):
                 plan.append((k, range(first, first + w_passes)))
 
+        loads = []
+        for k in range(STEPS):
+            for load in range(PASSES // LOAD_PASSES):
+                if k == 0:
+                    loads.append((None, load))
+                loads.append((k, load))
+
+        sorted_x = {}
+        sorted_w = {}
+
+        def load_and_sort(k, load):
+            if k is None:
+                sorted_x[load] = sort_halves(load_rows(x_loads, x_view, load), "x")
+            else:
+                w_view = W[k].rearrange("(p r) d -> p r d", r=BLOCKS)
+                sorted_w[(k, load)] = sort_halves(load_rows(w_loads, w_view, load), "w")
+
+        load_and_sort(*loads[0])
+        load_and_sort(*loads[1])
+        next_load = 2
+        to_quantise = []
         quantised = {}
         closed_in = {}
         for rnd in range(len(plan) + LAG + TIMES + 7):
@@ -270,25 +296,23 @@ def tile_infonceloss_pa_k_kernel(tc, embeddings, contexts, W, out):
             if rnd < len(plan):
                 k, w_passes = plan[rnd]
                 if k == 0:
-                    g = rnd
-                    if g % LOAD_PASSES == 0:
-                        x_raw = load_rows(x_loads, x_view, g // LOAD_PASSES)
-                    cols = slice(g * ROWS, (g + 1) * ROWS)
-                    turned.append((turn_pass(x_raw, g, False), x_codes[:, cols], x_scales[:, cols]))
+                    cols = slice(rnd * ROWS, (rnd + 1) * ROWS)
+                    turned.append((turn_pass(sorted_x[rnd // LOAD_PASSES], rnd), x_codes[:, cols], x_scales[:, cols]))
                 for g in w_passes:
-                    if g % LOAD_PASSES == 0:
-                        w_view = W[k].rearrange("(p r) d -> p r d", r=BLOCKS)
-                        w_raw = load_rows(w_loads, w_view, g // LOAD_PASSES)
                     w_codes = w_mx.tile([P, ROWS], U32, tag="w_codes", align_bytes=64)
                     w_scales = w_mx.tile([P, ROWS], U8, tag="w_scales", align_bytes=64)
-                    turned.append((turn_pass(w_raw, g, len(turned) == 1), w_codes[:], w_scales[:]))
+                    turned.append((turn_pass(sorted_w[(k, g // LOAD_PASSES)], g), w_codes[:], w_scales[:]))
                     quantised[rnd].append((k, g, w_codes, w_scales))
             for done in sorted(closed_in):
                 pair = rnd - closed_in[done] - 1
                 if 0 <= pair < pairs(done):
                     turned.append(turn_xw(done, pair))
-            for grouped, codes, scales in turned:
+            for grouped, codes, scales in to_quantise:
                 quantise(grouped, codes, scales)
+            to_quantise = turned
+            if next_load < len(loads):
+                load_and_sort(*loads[next_load])
+                next_load += 1
             for k, g, w_codes, w_scales in quantised.get(rnd - LAG, []):
                 multiply(k, g, w_codes, w_scales)
                 if g == PASSES - 1:
@@ -296,7 +320,7 @@ def tile_infonceloss_pa_k_kernel(tc, embeddings, contexts, W, out):
             for done in sorted(closed_in):
                 if rnd == closed_in[done]:
                     round_xw(done)
-                since_turned = rnd - closed_in[done] - pairs(done)
+                since_turned = rnd - closed_in[done] - pairs(done) - 1
                 if since_turned == 1:
                     score(done)
                 if since_turned == 2:

@@ -1,3 +1,4 @@
+import math
 from contextlib import ExitStack
 
 import concourse.mybir as mybir
@@ -26,7 +27,9 @@ LOAD_PASSES = 2
 LOAD_D = LOAD_PASSES * K_PASS
 PASS_WORDS = K_PASS // 2
 HALF_BLOCK = 8
+TURNS = 2
 LAG = 2
+LOSSES = 4 + 3 + 2
 GATHER = 8
 
 FLOPS = 2 * (4 + 3 + 2) * P * DY * DX + 2 * (4 + 3 + 2) * P * P * DY
@@ -38,11 +41,10 @@ def tile_infonceloss_pa_k_kernel(tc, embeddings, contexts, W, out):
     with ExitStack() as ctx:
         consts = ctx.enter_context(tc.tile_pool(name="consts", bufs=1))
         keep = ctx.enter_context(tc.tile_pool(name="keep", bufs=1))
-        x_loads = ctx.enter_context(tc.tile_pool(name="x_loads", bufs=3))
-        w_loads = ctx.enter_context(tc.tile_pool(name="w_loads", bufs=7))
-        sorted_loads = ctx.enter_context(tc.tile_pool(name="sorted_loads", bufs=2))
-        stage = ctx.enter_context(tc.tile_pool(name="stage", bufs=6))
-        w_mx = ctx.enter_context(tc.tile_pool(name="w_mx", bufs=2 * (LAG + 2)))
+        loads = ctx.enter_context(tc.tile_pool(name="loads", bufs=8))
+        sorted_loads = ctx.enter_context(tc.tile_pool(name="sorted_loads", bufs=4))
+        stage = ctx.enter_context(tc.tile_pool(name="stage", bufs=2 * TURNS + 2))
+        w_mx = ctx.enter_context(tc.tile_pool(name="w_mx", bufs=TURNS * (LAG + 2)))
         second = ctx.enter_context(tc.tile_pool(name="second", bufs=2))
         xw_rows = ctx.enter_context(tc.tile_pool(name="xw_rows", bufs=TIMES))
         e_stage = ctx.enter_context(tc.tile_pool(name="e_stage", bufs=2))
@@ -69,23 +71,28 @@ def tile_infonceloss_pa_k_kernel(tc, embeddings, contexts, W, out):
         warm = consts.tile([P, 1], F32)
         nc.scalar.activation(out=warm[:], in_=place[:, 0:1], func=ACT.Exp)
 
-        def load_rows(pool, rows_view, load):
-            raw = pool.tile([P, BLOCKS * LOAD_D], BF16, tag="raw")
+        def load_rows(rows_view, load):
+            raw = loads.tile([P, BLOCKS * LOAD_D], BF16, tag="raw")
             nc.sync.dma_start(
                 out=raw[:].rearrange("p (r d) -> p r d", r=BLOCKS),
                 in_=rows_view[:, :, load * LOAD_D : (load + 1) * LOAD_D],
             )
             return raw
 
-        def sort_halves(raw, tag):
-            halves = sorted_loads.tile([P, BLOCKS * LOAD_D], BF16, tag=tag)
-            nc.vector.tensor_copy(
-                out=halves[:].rearrange("p (rg u q i) -> p rg u q i", rg=BLOCKS * LOAD_PASSES, u=2, i=2 * HALF_BLOCK),
-                in_=raw[:].rearrange("p (rg q u i) -> p rg u q i", rg=BLOCKS * LOAD_PASSES, u=2, i=2 * HALF_BLOCK),
+        def load_pass(raw, rows_view, g):
+            half = raw[:, g * BLOCKS * K_PASS : (g + 1) * BLOCKS * K_PASS]
+            nc.sync.dma_start(
+                out=half.rearrange("p (r d) -> p r d", r=BLOCKS),
+                in_=rows_view[:, :, g * K_PASS : (g + 1) * K_PASS],
             )
-            return halves
 
-        def turn_pass(halves, g):
+        def sort_halves(halves, raw, cols):
+            nc.vector.tensor_copy(
+                out=halves[:, cols].rearrange("p (n u q i) -> p n u q i", u=2, q=K_PASS // 32, i=2 * HALF_BLOCK),
+                in_=raw[:, cols].rearrange("p (n q u i) -> p n u q i", u=2, q=K_PASS // 32, i=2 * HALF_BLOCK),
+            )
+
+        def turn_pass(halves, firsts):
             words = halves[:].bitcast(F32)
             grouped = stage.tile([P, ROWS * PACK], BF16, tag="grouped", align_bytes=64)
             grouped_words = grouped[:].bitcast(F32).rearrange("p (c u) -> p c u", u=2)
@@ -93,7 +100,7 @@ def tile_infonceloss_pa_k_kernel(tc, embeddings, contexts, W, out):
                 bank = work_psum.tile([P, 2, 2 * P], F32, tag="work")
                 for blk in range(2):
                     for u in range(2):
-                        first = ((2 * half + blk) * LOAD_PASSES + g % LOAD_PASSES) * PASS_WORDS + u * P
+                        first = firsts[2 * half + blk] + u * P
                         nc.tensor.transpose(
                             bank[:, u, blk * P : (blk + 1) * P], words[:, first : first + P], ident_f32[:]
                         )
@@ -124,17 +131,18 @@ def tile_infonceloss_pa_k_kernel(tc, embeddings, contexts, W, out):
         def pairs(k):
             return (TIMES - k + 1) // 2
 
+        def loss_cols(k):
+            first = sum(TIMES - j for j in range(k))
+            return slice(first, first + TIMES - k)
+
         xw = {}
         xw_codes = {}
         xw_scales = {}
         scores = {}
-        top = {}
-        minus_top = {}
-        top_less_positive = {}
-        exp_sums = {}
-        log_mean = {}
-        placed = {}
-        gathered = {}
+        minus_top = keep.tile([P, LOSSES], F32)
+        positive = keep.tile([P, LOSSES], F32)
+        exp_sums = keep.tile([P, LOSSES], F32)
+        offsets = keep.tile([P, LOSSES], F32)
 
         def round_xw(k):
             xw_codes[k] = second.tile([P, TIMES * P], U32, tag="xw_codes", align_bytes=64, name="xw_codes_%d" % k)
@@ -167,10 +175,23 @@ def tile_infonceloss_pa_k_kernel(tc, embeddings, contexts, W, out):
                     start=True,
                     stop=True,
                 )
-            top[k] = second.tile([P, n_s], F32, tag="top", name="top_%d" % k)
-            nc.vector.tensor_reduce(out=top[k][:], in_=scores[k][:], axis=AXIS.X, op=ALU.max)
-            minus_top[k] = second.tile([P, n_s], F32, tag="minus_top", name="minus_top_%d" % k)
-            nc.vector.tensor_scalar_mul(out=minus_top[k][:], in0=top[k][:], scalar1=-1.0)
+            top = second.tile([P, n_s], F32, tag="top")
+            nc.vector.tensor_reduce(out=top[:], in_=scores[k][:], axis=AXIS.X, op=ALU.max)
+            nc.vector.tensor_scalar_mul(out=minus_top[:, loss_cols(k)], in0=top[:], scalar1=-1.0)
+
+        def exponentials(k):
+            n_s = TIMES - k
+            exps = second.tile([P, n_s, P], F32, tag="exps")
+            first = loss_cols(k).start
+            for s in range(n_s):
+                nc.scalar.activation(
+                    out=exps[:, s, :],
+                    in_=scores[k][:, s, :],
+                    func=ACT.Exp,
+                    bias=minus_top[:, first + s : first + s + 1],
+                    scale=1.0,
+                    accum_out=exp_sums[:, first + s : first + s + 1],
+                )
 
         def diagonal(k):
             n_s = TIMES - k
@@ -181,65 +202,57 @@ def tile_infonceloss_pa_k_kernel(tc, embeddings, contexts, W, out):
                 in1=ident_f32[:].unsqueeze(1).to_broadcast([P, n_s, P]),
                 op=ALU.mult,
             )
-            positive = second.tile([P, n_s], F32, tag="positive")
-            nc.vector.tensor_reduce(out=positive[:], in_=on_diagonal[:], axis=AXIS.X, op=ALU.add)
-            top_less_positive[k] = second.tile([P, n_s], F32, tag="top_less_positive", name="tlp_%d" % k)
-            nc.vector.tensor_sub(out=top_less_positive[k][:], in0=top[k][:], in1=positive[:])
+            nc.vector.tensor_reduce(out=positive[:, loss_cols(k)], in_=on_diagonal[:], axis=AXIS.X, op=ALU.add)
+            least = second.tile([P, n_s], F32, tag="least")
+            nc.vector.tensor_scalar(
+                out=least[:],
+                in0=minus_top[:, loss_cols(k)],
+                scalar1=math.log(P * n_s),
+                scalar2=-1.0,
+                op0=ALU.add,
+                op1=ALU.mult,
+            )
+            nc.vector.tensor_sub(out=offsets[:, loss_cols(k)], in0=least[:], in1=positive[:, loss_cols(k)])
 
-        def exponentials(k):
-            n_s = TIMES - k
-            exps = second.tile([P, n_s, P], F32, tag="exps")
-            exp_sums[k] = second.tile([P, n_s], F32, tag="exp_sums", name="exp_sums_%d" % k)
-            for s in range(n_s):
-                nc.scalar.activation(
-                    out=exps[:, s, :],
-                    in_=scores[k][:, s, :],
-                    func=ACT.Exp,
-                    bias=minus_top[k][:, s : s + 1],
-                    scale=1.0,
-                    accum_out=exp_sums[k][:, s : s + 1],
+        def store_losses():
+            logs = keep.tile([P, LOSSES], F32)
+            nc.scalar.activation(out=logs[:], in_=exp_sums[:], func=ACT.Ln, scale=1.0)
+            loss = keep.tile([P, LOSSES], F32)
+            nc.vector.tensor_add(out=loss[:], in0=logs[:], in1=offsets[:])
+            placed = keep.tile([P, LOSSES * GATHER], F32)
+            for k in range(STEPS):
+                n_s = TIMES - k
+                first = loss_cols(k).start
+                nc.vector.tensor_tensor(
+                    out=placed[:, first * GATHER : (first + n_s) * GATHER].rearrange("p (l s) -> p l s", s=n_s),
+                    in0=place[:].unsqueeze(2).to_broadcast([P, GATHER, n_s]),
+                    in1=loss[:, loss_cols(k)].unsqueeze(1).to_broadcast([P, GATHER, n_s]),
+                    op=ALU.mult,
                 )
-
-        def logarithm(k):
-            n_s = TIMES - k
-            log_mean[k] = second.tile([P, n_s], F32, tag="log_mean", name="log_mean_%d" % k)
-            nc.scalar.activation(out=log_mean[k][:], in_=exp_sums[k][:], func=ACT.Ln, scale=1.0 / (P * n_s))
-
-        def place_loss(k):
-            n_s = TIMES - k
-            loss = second.tile([P, n_s], F32, tag="loss")
-            nc.vector.tensor_add(out=loss[:], in0=log_mean[k][:], in1=top_less_positive[k][:])
-            placed[k] = second.tile([P, GATHER, n_s], F32, tag="placed", name="placed_%d" % k)
-            nc.vector.tensor_tensor(
-                out=placed[k][:],
-                in0=place[:].unsqueeze(2).to_broadcast([P, GATHER, n_s]),
-                in1=loss[:].unsqueeze(1).to_broadcast([P, GATHER, n_s]),
-                op=ALU.mult,
-            )
-
-        def gather(k):
-            gathered[k] = sums_psum.tile([P, GATHER * (TIMES - k)], F32, tag=own_bank(k), name="gathered_%d" % k)
-            nc.tensor.matmul(
-                out=gathered[k][:], lhsT=group[:], rhs=placed[k][:].rearrange("p l s -> p (l s)"), start=True, stop=True
-            )
-
-        def store(k):
+            gathered = sums_psum.tile([P, LOSSES * GATHER], F32, tag=own_bank(0))
+            nc.tensor.matmul(out=gathered[:], lhsT=group[:], rhs=placed[:], start=True, stop=True)
             groups = P // GATHER
-            n = GATHER * (TIMES - k)
-            runs = second.tile([groups, n], F32, tag="runs")
-            nc.scalar.copy(out=runs[:], in_=gathered[k][0:groups, :])
-            first = sum(P * (TIMES - j) for j in range(k))
-            nc.scalar.dma_start(out=out[first : first + groups * n].rearrange("(h n) -> h n", h=groups), in_=runs[:])
+            runs = keep.tile([groups, LOSSES * GATHER], F32)
+            nc.scalar.copy(out=runs[:], in_=gathered[0:groups, :])
+            for k in range(STEPS):
+                n_s = TIMES - k
+                first = loss_cols(k).start
+                queue = nc.scalar if k % 2 == 0 else nc.sync
+                queue.dma_start(
+                    out=out[first * P : (first + n_s) * P].rearrange("(h n) -> h n", h=groups),
+                    in_=runs[:, first * GATHER : (first + n_s) * GATHER],
+                )
 
         c_raw = keep.tile([P, TIMES * DY], BF16)
         nc.sync.dma_start(out=c_raw[:].rearrange("p (t e) -> p t e", t=TIMES), in_=contexts[:, 0:TIMES, :])
         c_codes = keep.tile([P, TIMES * P], U32, align_bytes=64)
         c_scales = keep.tile([P, TIMES * P], U8, align_bytes=64)
         c_rows = [c_raw[:, s * DY : (s + 1) * DY].rearrange("b (p t) -> b t p", t=PACK) for s in range(TIMES)]
-        c_turned = [turn_rows(c_rows[2 * pair : 2 * pair + 2], "sums%d" % pair, pair % 2 == 1) for pair in range(2)]
+        to_quantise = []
         for pair in range(2):
             cols = slice(2 * pair * P, 2 * (pair + 1) * P)
-            quantise(c_turned[pair], c_codes[:, cols], c_scales[:, cols])
+            grouped = turn_rows(c_rows[2 * pair : 2 * pair + 2], "sums%d" % pair, True)
+            to_quantise.append((grouped, c_codes[:, cols], c_scales[:, cols]))
 
         x_view = embeddings[:, 1 : 1 + TIMES, :]
         x_codes = keep.tile([P, PASSES * ROWS], U32, align_bytes=64)
@@ -261,76 +274,90 @@ def tile_infonceloss_pa_k_kernel(tc, embeddings, contexts, W, out):
                     stop=(g == PASSES - 1),
                 )
 
-        plan = []
+        turns = []
         for k in range(STEPS):
-            w_passes = 1 if k == 0 else 2
-            for first in range(0, PASSES, w_passes):
-                plan.append((k, range(first, first + w_passes)))
-
-        loads = []
-        for k in range(STEPS):
-            for load in range(PASSES // LOAD_PASSES):
+            for g in range(PASSES):
                 if k == 0:
-                    loads.append((None, load))
-                loads.append((k, load))
+                    turns.append((None, g))
+                turns.append((k, g))
+        rounds = [turns[first : first + TURNS] for first in range(0, len(turns), TURNS)]
 
-        sorted_x = {}
-        sorted_w = {}
+        def view(k):
+            return x_view if k is None else W[k].rearrange("(p r) d -> p r d", r=BLOCKS)
+
+        load_order = []
+        for k, g in turns:
+            if (k, g // LOAD_PASSES) not in load_order:
+                load_order.append((k, g // LOAD_PASSES))
+        halves_of = {}
+        firsts_of = {}
+
+        def sorted_tile(k, load):
+            halves_of[(k, load)] = sorted_loads.tile(
+                [P, BLOCKS * LOAD_D], BF16, tag="halves", name="halves_%s_%d" % (k, load)
+            )
+            return halves_of[(k, load)]
+
+        first_loads = load_order[:2]
+        raws = [loads.tile([P, BLOCKS * LOAD_D], BF16, tag="raw", name="raw_first_%d" % i) for i in range(2)]
+        tiles = [sorted_tile(k, load) for k, load in first_loads]
+        for g in range(LOAD_PASSES):
+            for (k, load), raw, halves in zip(first_loads, raws, tiles):
+                load_pass(raw, view(k), g)
+                sort_halves(halves, raw, slice(g * BLOCKS * K_PASS, (g + 1) * BLOCKS * K_PASS))
+                firsts_of[(k, g)] = [(g * BLOCKS + r) * PASS_WORDS for r in range(BLOCKS)]
 
         def load_and_sort(k, load):
-            if k is None:
-                sorted_x[load] = sort_halves(load_rows(x_loads, x_view, load), "x")
-            else:
-                w_view = W[k].rearrange("(p r) d -> p r d", r=BLOCKS)
-                sorted_w[(k, load)] = sort_halves(load_rows(w_loads, w_view, load), "w")
+            raw = load_rows(view(k), load)
+            sort_halves(sorted_tile(k, load), raw, slice(0, BLOCKS * LOAD_D))
+            for g in range(LOAD_PASSES):
+                firsts_of[(k, load * LOAD_PASSES + g)] = [(r * LOAD_PASSES + g) * PASS_WORDS for r in range(BLOCKS)]
 
-        load_and_sort(*loads[0])
-        load_and_sort(*loads[1])
-        next_load = 2
-        to_quantise = []
+        pieces = {}
+
+        def plan_second(k, rnd):
+            todo = [[lambda: to_quantise.append(turn_xw(k, 0))]]
+            if pairs(k) == 2:
+                todo += [[lambda: to_quantise.append(turn_xw(k, 1))], []]
+            todo += [[], [], [lambda: score(k)], [lambda: exponentials(k)], [lambda: diagonal(k)]]
+            if k == STEPS - 1:
+                todo += [[store_losses]]
+            for i, functions in enumerate(todo):
+                at = 2 * (rnd + 1) + 1 + i
+                pieces.setdefault((at // 2, at % 2), []).extend(functions)
+
+        def work_pieces(rnd, place):
+            for piece in pieces.get((rnd, place), []):
+                piece()
+
+        n_sorted = 2
         quantised = {}
-        closed_in = {}
-        for rnd in range(len(plan) + LAG + TIMES + 7):
-            turned = []
+        for rnd in range(len(rounds) + LAG + 4):
+            now_quantised = to_quantise
+            to_quantise = []
+            work_pieces(rnd, 0)
             quantised[rnd] = []
-            if rnd < len(plan):
-                k, w_passes = plan[rnd]
-                if k == 0:
-                    cols = slice(rnd * ROWS, (rnd + 1) * ROWS)
-                    turned.append((turn_pass(sorted_x[rnd // LOAD_PASSES], rnd), x_codes[:, cols], x_scales[:, cols]))
-                for g in w_passes:
+            for k, g in rounds[rnd] if rnd < len(rounds) else []:
+                grouped = turn_pass(halves_of[(k, g // LOAD_PASSES)], firsts_of[(k, g)])
+                if k is None:
+                    cols = slice(g * ROWS, (g + 1) * ROWS)
+                    to_quantise.append((grouped, x_codes[:, cols], x_scales[:, cols]))
+                else:
                     w_codes = w_mx.tile([P, ROWS], U32, tag="w_codes", align_bytes=64)
                     w_scales = w_mx.tile([P, ROWS], U8, tag="w_scales", align_bytes=64)
-                    turned.append((turn_pass(sorted_w[(k, g // LOAD_PASSES)], g), w_codes[:], w_scales[:]))
+                    to_quantise.append((grouped, w_codes[:], w_scales[:]))
                     quantised[rnd].append((k, g, w_codes, w_scales))
-            for done in sorted(closed_in):
-                pair = rnd - closed_in[done] - 1
-                if 0 <= pair < pairs(done):
-                    turned.append(turn_xw(done, pair))
-            for grouped, codes, scales in to_quantise:
+            work_pieces(rnd, 1)
+            for grouped, codes, scales in now_quantised:
                 quantise(grouped, codes, scales)
-            to_quantise = turned
-            if next_load < len(loads):
-                load_and_sort(*loads[next_load])
-                next_load += 1
+            ahead = 2 + (rnd + 1) * TURNS // LOAD_PASSES
+            for k, g in rounds[rnd + 1] if rnd + 1 < len(rounds) else []:
+                ahead = max(ahead, load_order.index((k, g // LOAD_PASSES)) + 1)
+            for k, load in load_order[n_sorted:ahead]:
+                load_and_sort(k, load)
+            n_sorted = max(n_sorted, ahead)
             for k, g, w_codes, w_scales in quantised.get(rnd - LAG, []):
                 multiply(k, g, w_codes, w_scales)
                 if g == PASSES - 1:
-                    closed_in[k] = rnd
-            for done in sorted(closed_in):
-                if rnd == closed_in[done]:
-                    round_xw(done)
-                since_turned = rnd - closed_in[done] - pairs(done) - 1
-                if since_turned == 1:
-                    score(done)
-                if since_turned == 2:
-                    exponentials(done)
-                if since_turned == 3:
-                    logarithm(done)
-                    diagonal(done)
-                if since_turned == 4:
-                    place_loss(done)
-                if since_turned == 5:
-                    gather(done)
-                if since_turned == 6:
-                    store(done)
+                    round_xw(k)
+                    plan_second(k, rnd)

@@ -92,44 +92,45 @@ def tile_infonceloss_pa_k_kernel(tc, embeddings, contexts, W, out):
                 in_=raw[:, cols].rearrange("p (n q u i) -> p n u q i", u=2, q=K_PASS // 32, i=2 * HALF_BLOCK),
             )
 
-        def turn_pass(halves, firsts):
-            words = halves[:].bitcast(F32)
+        def turn_pass(words):
             grouped = stage.tile([P, ROWS * PACK], BF16, tag="grouped", align_bytes=64)
             grouped_words = grouped[:].bitcast(F32).rearrange("p (c u) -> p c u", u=2)
             for half in range(2):
                 bank = work_psum.tile([P, 2, 2 * P], F32, tag="work")
                 for blk in range(2):
                     for u in range(2):
-                        first = firsts[2 * half + blk] + u * P
                         nc.tensor.transpose(
-                            bank[:, u, blk * P : (blk + 1) * P], words[:, first : first + P], ident_f32[:]
+                            bank[:, u, blk * P : (blk + 1) * P], words[2 * half + blk][u], ident_f32[:]
                         )
                 side_by_side = grouped_words[:, half * 2 * P : (half + 1) * 2 * P, :]
                 nc.scalar.copy(out=side_by_side, in_=bank[:].rearrange("p u c -> p c u"))
             return grouped
 
+        def sorted_words(halves, firsts):
+            words = halves[:].bitcast(F32)
+            return [[words[:, first + u * P : first + (u + 1) * P] for u in range(2)] for first in firsts]
+
         def quantise(grouped, codes, scales):
             nc.vector.quantize_mx(out=codes.bitcast(FP8X4), scales=scales, in_=grouped[:])
 
-        def turn_rows(rows_list, bank, on_scalar):
-            n = len(rows_list)
+        def turn_xw(k, times, bank, on_scalar):
+            n = len(times)
+            cols = slice(times[0] * P, (times[-1] + 1) * P)
             turned = sums_psum.tile([P, n, PACK, P], BF16, tag=bank)
             for i in range(n):
                 for t in range(PACK):
-                    nc.tensor.transpose(turned[:, i, t, :], rows_list[i][:, t, :], ident_bf16[:])
+                    rows = xw[(k, times[i])][:, t * P : (t + 1) * P]
+                    nc.tensor.transpose(turned[:, i, t, :], rows, ident_bf16[:])
             grouped = e_stage.tile([P, n * P * PACK], BF16, tag="grouped_e", align_bytes=64)
             side_by_side = grouped[:].rearrange("p (i r t) -> p i r t", i=n, t=PACK)
             if on_scalar:
                 nc.scalar.copy(out=side_by_side, in_=turned[:].rearrange("p i t r -> p i r t"))
             else:
                 nc.vector.tensor_copy(out=side_by_side, in_=turned[:].rearrange("p i t r -> p i r t"))
-            return grouped
+            return (grouped, xw_codes[k][:, cols], xw_scales[k][:, cols])
 
         def own_bank(k):
             return "sums%d" % (TIMES - 1 - k)
-
-        def pairs(k):
-            return (TIMES - k + 1) // 2
 
         def loss_cols(k):
             first = sum(TIMES - j for j in range(k))
@@ -154,13 +155,6 @@ def tile_infonceloss_pa_k_kernel(tc, embeddings, contexts, W, out):
                 else:
                     nc.vector.tensor_copy(out=xw[(k, s)][:], in_=sums[(k, s)][:])
 
-        def turn_xw(k, pair):
-            times = range(2 * pair, min(2 * pair + 2, TIMES - k))
-            cols = slice(times[0] * P, (times[-1] + 1) * P)
-            rows = [xw[(k, s)][:].rearrange("b (t p) -> b t p", t=PACK) for s in times]
-            grouped = turn_rows(rows, own_bank(k), pair % 2 == 1)
-            return (grouped, xw_codes[k][:, cols], xw_scales[k][:, cols])
-
         def score(k):
             n_s = TIMES - k
             scores[k] = sums_psum.tile([P, n_s, P], F32, tag=own_bank(k), name="scores_%d" % k)
@@ -175,9 +169,9 @@ def tile_infonceloss_pa_k_kernel(tc, embeddings, contexts, W, out):
                     start=True,
                     stop=True,
                 )
-            top = second.tile([P, n_s], F32, tag="top")
-            nc.vector.tensor_reduce(out=top[:], in_=scores[k][:], axis=AXIS.X, op=ALU.max)
-            nc.vector.tensor_scalar_mul(out=minus_top[:, loss_cols(k)], in0=top[:], scalar1=-1.0)
+            nc.vector.tensor_reduce(
+                out=minus_top[:, loss_cols(k)], in_=scores[k][:], axis=AXIS.X, op=ALU.max, negate=True
+            )
 
         def exponentials(k):
             n_s = TIMES - k
@@ -247,12 +241,9 @@ def tile_infonceloss_pa_k_kernel(tc, embeddings, contexts, W, out):
         nc.sync.dma_start(out=c_raw[:].rearrange("p (t e) -> p t e", t=TIMES), in_=contexts[:, 0:TIMES, :])
         c_codes = keep.tile([P, TIMES * P], U32, align_bytes=64)
         c_scales = keep.tile([P, TIMES * P], U8, align_bytes=64)
-        c_rows = [c_raw[:, s * DY : (s + 1) * DY].rearrange("b (p t) -> b t p", t=PACK) for s in range(TIMES)]
-        to_quantise = []
-        for pair in range(2):
-            cols = slice(2 * pair * P, 2 * (pair + 1) * P)
-            grouped = turn_rows(c_rows[2 * pair : 2 * pair + 2], "sums%d" % pair, True)
-            to_quantise.append((grouped, c_codes[:, cols], c_scales[:, cols]))
+        c_words = c_raw[:].bitcast(F32).rearrange("b (t p u) -> b t u p", t=TIMES, u=2)
+        c_turned = turn_pass([[c_words[:, t, u, :] for u in range(2)] for t in range(TIMES)])
+        to_quantise = [(c_turned, c_codes[:], c_scales[:])]
 
         x_view = embeddings[:, 1 : 1 + TIMES, :]
         x_codes = keep.tile([P, PASSES * ROWS], U32, align_bytes=64)
@@ -316,9 +307,17 @@ def tile_infonceloss_pa_k_kernel(tc, embeddings, contexts, W, out):
         pieces = {}
 
         def plan_second(k, rnd):
-            todo = [[lambda: to_quantise.append(turn_xw(k, 0))]]
-            if pairs(k) == 2:
-                todo += [[lambda: to_quantise.append(turn_xw(k, 1))], []]
+            if k < STEPS - 1:
+                halves = [range(first, min(first + 2, TIMES - k)) for first in range(0, TIMES - k, 2)]
+                todo = [[lambda: to_quantise.append(turn_xw(k, halves[0], own_bank(k), False))]]
+                todo += [[lambda: to_quantise.append(turn_xw(k, halves[1], own_bank(k), True))], []]
+            else:
+                todo = [
+                    [
+                        lambda: to_quantise.append(turn_xw(k, [0], own_bank(0), True)),
+                        lambda: to_quantise.append(turn_xw(k, [1], own_bank(k), False)),
+                    ]
+                ]
             todo += [[], [], [lambda: score(k)], [lambda: exponentials(k)], [lambda: diagonal(k)]]
             if k == STEPS - 1:
                 todo += [[store_losses]]
@@ -338,7 +337,7 @@ def tile_infonceloss_pa_k_kernel(tc, embeddings, contexts, W, out):
             work_pieces(rnd, 0)
             quantised[rnd] = []
             for k, g in rounds[rnd] if rnd < len(rounds) else []:
-                grouped = turn_pass(halves_of[(k, g // LOAD_PASSES)], firsts_of[(k, g)])
+                grouped = turn_pass(sorted_words(halves_of[(k, g // LOAD_PASSES)], firsts_of[(k, g)]))
                 if k is None:
                     cols = slice(g * ROWS, (g + 1) * ROWS)
                     to_quantise.append((grouped, x_codes[:, cols], x_scales[:, cols]))

@@ -28,7 +28,10 @@ LOAD_D = LOAD_PASSES * K_PASS
 PASS_WORDS = K_PASS // 2
 HALF_BLOCK = 8
 TURNS = 2
+SINGLE = 6
 LAG = 2
+ALONE = 24
+CONTEXTS_ROUND = 14
 LOSSES = 4 + 3 + 2
 GATHER = 8
 
@@ -41,7 +44,7 @@ def tile_infonceloss_pa_k_kernel(tc, embeddings, contexts, W, out):
     with ExitStack() as ctx:
         consts = ctx.enter_context(tc.tile_pool(name="consts", bufs=1))
         keep = ctx.enter_context(tc.tile_pool(name="keep", bufs=1))
-        loads = ctx.enter_context(tc.tile_pool(name="loads", bufs=8))
+        loads = ctx.enter_context(tc.tile_pool(name="loads", bufs=7))
         sorted_loads = ctx.enter_context(tc.tile_pool(name="sorted_loads", bufs=4))
         stage = ctx.enter_context(tc.tile_pool(name="stage", bufs=2 * TURNS + 2))
         w_mx = ctx.enter_context(tc.tile_pool(name="w_mx", bufs=TURNS * (LAG + 2)))
@@ -71,16 +74,15 @@ def tile_infonceloss_pa_k_kernel(tc, embeddings, contexts, W, out):
         warm = consts.tile([P, 1], F32)
         nc.scalar.activation(out=warm[:], in_=place[:, 0:1], func=ACT.Exp)
 
-        def load_rows(rows_view, load):
-            raw = loads.tile([P, BLOCKS * LOAD_D], BF16, tag="raw")
+        def load_rows(raw, rows_view, load):
             nc.sync.dma_start(
                 out=raw[:].rearrange("p (r d) -> p r d", r=BLOCKS),
                 in_=rows_view[:, :, load * LOAD_D : (load + 1) * LOAD_D],
             )
-            return raw
 
         def load_pass(raw, rows_view, g):
-            half = raw[:, g * BLOCKS * K_PASS : (g + 1) * BLOCKS * K_PASS]
+            i = g % LOAD_PASSES
+            half = raw[:, i * BLOCKS * K_PASS : (i + 1) * BLOCKS * K_PASS]
             nc.sync.dma_start(
                 out=half.rearrange("p (r d) -> p r d", r=BLOCKS),
                 in_=rows_view[:, :, g * K_PASS : (g + 1) * K_PASS],
@@ -237,13 +239,18 @@ def tile_infonceloss_pa_k_kernel(tc, embeddings, contexts, W, out):
                     in_=runs[:, first * GATHER : (first + n_s) * GATHER],
                 )
 
-        c_raw = keep.tile([P, TIMES * DY], BF16)
-        nc.sync.dma_start(out=c_raw[:].rearrange("p (t e) -> p t e", t=TIMES), in_=contexts[:, 0:TIMES, :])
         c_codes = keep.tile([P, TIMES * P], U32, align_bytes=64)
         c_scales = keep.tile([P, TIMES * P], U8, align_bytes=64)
-        c_words = c_raw[:].bitcast(F32).rearrange("b (t p u) -> b t u p", t=TIMES, u=2)
-        c_turned = turn_pass([[c_words[:, t, u, :] for u in range(2)] for t in range(TIMES)])
-        to_quantise = [(c_turned, c_codes[:], c_scales[:])]
+
+        def load_contexts():
+            c_raw = keep.tile([P, TIMES * DY], BF16, name="c_raw")
+            nc.sync.dma_start(out=c_raw[:].rearrange("p (t e) -> p t e", t=TIMES), in_=contexts[:, 0:TIMES, :])
+            return c_raw
+
+        def turn_contexts(c_raw):
+            words = c_raw[:].bitcast(F32).rearrange("b (t p u) -> b t u p", t=TIMES, u=2)
+            turned = turn_pass([[words[:, t, u, :] for u in range(2)] for t in range(TIMES)])
+            return (turned, c_codes[:], c_scales[:])
 
         x_view = embeddings[:, 1 : 1 + TIMES, :]
         x_codes = keep.tile([P, PASSES * ROWS], U32, align_bytes=64)
@@ -271,46 +278,56 @@ def tile_infonceloss_pa_k_kernel(tc, embeddings, contexts, W, out):
                 if k == 0:
                     turns.append((None, g))
                 turns.append((k, g))
-        rounds = [turns[first : first + TURNS] for first in range(0, len(turns), TURNS)]
+        starts = list(range(SINGLE)) + list(range(SINGLE, len(turns), TURNS))
+        rounds = [turns[first:after] for first, after in zip(starts, starts[1:] + [len(turns)])]
 
         def view(k):
             return x_view if k is None else W[k].rearrange("(p r) d -> p r d", r=BLOCKS)
 
-        load_order = []
-        for k, g in turns:
-            if (k, g // LOAD_PASSES) not in load_order:
-                load_order.append((k, g // LOAD_PASSES))
         halves_of = {}
         firsts_of = {}
 
-        def sorted_tile(k, load):
-            halves_of[(k, load)] = sorted_loads.tile(
-                [P, BLOCKS * LOAD_D], BF16, tag="halves", name="halves_%s_%d" % (k, load)
-            )
-            return halves_of[(k, load)]
+        raws = {}
 
-        first_loads = load_order[:2]
-        raws = [loads.tile([P, BLOCKS * LOAD_D], BF16, tag="raw", name="raw_first_%d" % i) for i in range(2)]
-        tiles = [sorted_tile(k, load) for k, load in first_loads]
-        for g in range(LOAD_PASSES):
-            for (k, load), raw, halves in zip(first_loads, raws, tiles):
-                load_pass(raw, view(k), g)
-                sort_halves(halves, raw, slice(g * BLOCKS * K_PASS, (g + 1) * BLOCKS * K_PASS))
-                firsts_of[(k, g)] = [(g * BLOCKS + r) * PASS_WORDS for r in range(BLOCKS)]
+        def load(k, g):
+            key = (k, g // LOAD_PASSES)
+            alone = turns.index((k, g)) < ALONE
+            if key not in raws:
+                raws[key] = loads.tile([P, BLOCKS * LOAD_D], BF16, tag="raw", name="raw_%s_%d" % key)
+                halves_of[key] = sorted_loads.tile([P, BLOCKS * LOAD_D], BF16, tag="halves", name="halves_%s_%d" % key)
+                if not alone:
+                    load_rows(raws[key], view(k), key[1])
+            if alone:
+                load_pass(raws[key], view(k), g)
+            return alone
 
-        def load_and_sort(k, load):
-            raw = load_rows(view(k), load)
-            sort_halves(sorted_tile(k, load), raw, slice(0, BLOCKS * LOAD_D))
-            for g in range(LOAD_PASSES):
-                firsts_of[(k, load * LOAD_PASSES + g)] = [(r * LOAD_PASSES + g) * PASS_WORDS for r in range(BLOCKS)]
+        def load_and_sort(k, g):
+            key = (k, g // LOAD_PASSES)
+            i = g % LOAD_PASSES
+            if load(k, g):
+                cols = slice(i * BLOCKS * K_PASS, (i + 1) * BLOCKS * K_PASS)
+                firsts_of[(k, g)] = [(i * BLOCKS + r) * PASS_WORDS for r in range(BLOCKS)]
+            else:
+                cols = slice(0, BLOCKS * LOAD_D)
+                for j in range(LOAD_PASSES):
+                    firsts_of[(k, g - i + j)] = [(r * LOAD_PASSES + j) * PASS_WORDS for r in range(BLOCKS)]
+            sort_halves(halves_of[key], raws[key], cols)
 
+        def sort_ahead(n):
+            for k, g in turns[:n]:
+                if (k, g) not in firsts_of:
+                    load_and_sort(k, g)
+
+        sort_ahead(starts[1] + 1)
+
+        to_quantise = []
         pieces = {}
 
         def plan_second(k, rnd):
             if k < STEPS - 1:
                 halves = [range(first, min(first + 2, TIMES - k)) for first in range(0, TIMES - k, 2)]
-                todo = [[lambda: to_quantise.append(turn_xw(k, halves[0], own_bank(k), False))]]
-                todo += [[lambda: to_quantise.append(turn_xw(k, halves[1], own_bank(k), True))], []]
+                todo = [[lambda: to_quantise.append(turn_xw(k, halves[0], own_bank(k), True))]]
+                todo += [[], [lambda: to_quantise.append(turn_xw(k, halves[1], own_bank(k), True))]]
             else:
                 todo = [
                     [
@@ -329,7 +346,7 @@ def tile_infonceloss_pa_k_kernel(tc, embeddings, contexts, W, out):
             for piece in pieces.get((rnd, place), []):
                 piece()
 
-        n_sorted = 2
+        to_multiply = []
         quantised = {}
         for rnd in range(len(rounds) + LAG + 4):
             now_quantised = to_quantise
@@ -346,17 +363,20 @@ def tile_infonceloss_pa_k_kernel(tc, embeddings, contexts, W, out):
                     w_scales = w_mx.tile([P, ROWS], U8, tag="w_scales", align_bytes=64)
                     to_quantise.append((grouped, w_codes[:], w_scales[:]))
                     quantised[rnd].append((k, g, w_codes, w_scales))
+            if rnd == CONTEXTS_ROUND - 2:
+                c_raw = load_contexts()
+            if rnd == CONTEXTS_ROUND:
+                to_quantise.append(turn_contexts(c_raw))
             work_pieces(rnd, 1)
             for grouped, codes, scales in now_quantised:
                 quantise(grouped, codes, scales)
-            ahead = 2 + (rnd + 1) * TURNS // LOAD_PASSES
-            for k, g in rounds[rnd + 1] if rnd + 1 < len(rounds) else []:
-                ahead = max(ahead, load_order.index((k, g // LOAD_PASSES)) + 1)
-            for k, load in load_order[n_sorted:ahead]:
-                load_and_sort(k, load)
-            n_sorted = max(n_sorted, ahead)
-            for k, g, w_codes, w_scales in quantised.get(rnd - LAG, []):
+            sort_ahead(starts[rnd + 2] + 1 if rnd + 2 < len(rounds) else len(turns))
+            to_multiply += quantised.get(rnd - LAG, [])
+            while to_multiply:
+                k, g, w_codes, w_scales = to_multiply[0]
+                to_multiply = to_multiply[1:]
                 multiply(k, g, w_codes, w_scales)
                 if g == PASSES - 1:
                     round_xw(k)
                     plan_second(k, rnd)
+                    break

@@ -32,6 +32,7 @@ SINGLE = 6
 LAG = 2
 ALONE = 24
 CONTEXTS_ROUND = 14
+IDLE_PRODUCTS = 5
 LOSSES = 4 + 3 + 2
 GATHER = 8
 
@@ -54,6 +55,12 @@ def tile_infonceloss_pa_k_kernel(tc, embeddings, contexts, W, out):
         sums_psum = ctx.enter_context(tc.psum_pool(name="sums_psum", bufs=1))
         work_psum = ctx.enter_context(tc.psum_pool(name="work_psum", bufs=4))
         ctx.enter_context(tc.manual_schedule())
+
+        zeros = consts.tile([P, DY], BF16)
+        nc.vector.memset(zeros[:], 0.0)
+        for i in range(IDLE_PRODUCTS):
+            unused = work_psum.tile([P, DY], F32, tag="work", name="unused")
+            nc.tensor.matmul(out=unused[:], lhsT=zeros[:, 0:P], rhs=zeros[:], start=True, stop=True)
 
         ident_f32 = consts.tile([P, P], F32)
         make_identity(nc, ident_f32[:])
@@ -115,7 +122,7 @@ def tile_infonceloss_pa_k_kernel(tc, embeddings, contexts, W, out):
         def quantise(grouped, codes, scales):
             nc.vector.quantize_mx(out=codes.bitcast(FP8X4), scales=scales, in_=grouped[:])
 
-        def turn_xw(k, times, bank, on_scalar):
+        def turn_xw(k, times, bank):
             n = len(times)
             cols = slice(times[0] * P, (times[-1] + 1) * P)
             turned = sums_psum.tile([P, n, PACK, P], BF16, tag=bank)
@@ -125,18 +132,15 @@ def tile_infonceloss_pa_k_kernel(tc, embeddings, contexts, W, out):
                     nc.tensor.transpose(turned[:, i, t, :], rows, ident_bf16[:])
             grouped = e_stage.tile([P, n * P * PACK], BF16, tag="grouped_e", align_bytes=64)
             side_by_side = grouped[:].rearrange("p (i r t) -> p i r t", i=n, t=PACK)
-            if on_scalar:
-                nc.scalar.copy(out=side_by_side, in_=turned[:].rearrange("p i t r -> p i r t"))
-            else:
-                nc.vector.tensor_copy(out=side_by_side, in_=turned[:].rearrange("p i t r -> p i r t"))
+            nc.scalar.copy(out=side_by_side, in_=turned[:].rearrange("p i t r -> p i r t"))
             return (grouped, xw_codes[k][:, cols], xw_scales[k][:, cols])
 
         def own_bank(k):
             return "sums%d" % (TIMES - 1 - k)
 
-        def loss_cols(k):
-            first = sum(TIMES - j for j in range(k))
-            return slice(first, first + TIMES - k)
+        def loss_cols(k, times):
+            first = sum(TIMES - j for j in range(k)) + times[0]
+            return slice(first, first + len(times))
 
         xw = {}
         xw_codes = {}
@@ -147,23 +151,27 @@ def tile_infonceloss_pa_k_kernel(tc, embeddings, contexts, W, out):
         exp_sums = keep.tile([P, LOSSES], F32)
         offsets = keep.tile([P, LOSSES], F32)
 
-        def round_xw(k):
+        placed_offsets = keep.tile([P, LOSSES * GATHER], F32)
+
+        def prepare_xw(k):
             xw_codes[k] = second.tile([P, TIMES * P], U32, tag="xw_codes", align_bytes=64, name="xw_codes_%d" % k)
             xw_scales[k] = second.tile([P, TIMES * P], U8, tag="xw_scales", align_bytes=64, name="xw_scales_%d" % k)
-            for s in range(TIMES - k):
-                xw[(k, s)] = xw_rows.tile([P, DY], BF16, tag="xw", name="xw_%d_%d" % (k, s))
-                if s % 2 == 0:
-                    nc.scalar.copy(out=xw[(k, s)][:], in_=sums[(k, s)][:])
-                else:
-                    nc.vector.tensor_copy(out=xw[(k, s)][:], in_=sums[(k, s)][:])
 
-        def score(k):
-            n_s = TIMES - k
-            scores[k] = sums_psum.tile([P, n_s, P], F32, tag=own_bank(k), name="scores_%d" % k)
-            for s in range(n_s):
-                cols = slice(s * P, (s + 1) * P)
+        def round_xw(k, s):
+            xw[(k, s)] = xw_rows.tile([P, DY], BF16, tag="xw", name="xw_%d_%d" % (k, s))
+            if s % 2 == 0:
+                nc.scalar.copy(out=xw[(k, s)][:], in_=sums[(k, s)][:])
+            else:
+                nc.vector.tensor_copy(out=xw[(k, s)][:], in_=sums[(k, s)][:])
+
+        def score(k, times, bank):
+            n = len(times)
+            found = sums_psum.tile([P, n, P], F32, tag=bank, name="scores_%d_%d" % (k, times[0]))
+            scores[(k, times[0])] = found
+            for i in range(n):
+                cols = slice(times[i] * P, (times[i] + 1) * P)
                 nc.tensor.matmul_mx(
-                    out=scores[k][:, s, :],
+                    out=found[:, i, :],
                     lhsT=xw_codes[k][:, cols].bitcast(FP8X4),
                     lhsT_scale=xw_scales[k][:, cols],
                     rhs=c_codes[:, cols].bitcast(FP8X4),
@@ -172,67 +180,76 @@ def tile_infonceloss_pa_k_kernel(tc, embeddings, contexts, W, out):
                     stop=True,
                 )
             nc.vector.tensor_reduce(
-                out=minus_top[:, loss_cols(k)], in_=scores[k][:], axis=AXIS.X, op=ALU.max, negate=True
+                out=minus_top[:, loss_cols(k, times)], in_=found[:], axis=AXIS.X, op=ALU.max, negate=True
             )
 
-        def exponentials(k):
-            n_s = TIMES - k
-            exps = second.tile([P, n_s, P], F32, tag="exps")
-            first = loss_cols(k).start
-            for s in range(n_s):
+        def exponentials(k, times):
+            exps = second.tile([P, len(times), P], F32, tag="exps")
+            for i in range(len(times)):
+                col = loss_cols(k, times[i : i + 1])
                 nc.scalar.activation(
-                    out=exps[:, s, :],
-                    in_=scores[k][:, s, :],
+                    out=exps[:, i, :],
+                    in_=scores[(k, times[0])][:, i, :],
                     func=ACT.Exp,
-                    bias=minus_top[:, first + s : first + s + 1],
+                    bias=minus_top[:, col],
                     scale=1.0,
-                    accum_out=exp_sums[:, first + s : first + s + 1],
+                    accum_out=exp_sums[:, col],
                 )
 
-        def diagonal(k):
-            n_s = TIMES - k
-            on_diagonal = second.tile([P, n_s, P], F32, tag="on_diagonal")
-            nc.vector.tensor_tensor(
-                out=on_diagonal[:],
-                in0=scores[k][:],
-                in1=ident_f32[:].unsqueeze(1).to_broadcast([P, n_s, P]),
-                op=ALU.mult,
-            )
-            nc.vector.tensor_reduce(out=positive[:, loss_cols(k)], in_=on_diagonal[:], axis=AXIS.X, op=ALU.add)
-            least = second.tile([P, n_s], F32, tag="least")
+        def diagonal(k, groups):
+            products = []
+            for times in groups:
+                n = len(times)
+                on_diagonal = second.tile([P, n, P], F32, tag="on_diagonal")
+                nc.vector.tensor_tensor(
+                    out=on_diagonal[:],
+                    in0=scores[(k, times[0])][:],
+                    in1=ident_f32[:].unsqueeze(1).to_broadcast([P, n, P]),
+                    op=ALU.mult,
+                )
+                products.append(on_diagonal)
+            cols = loss_cols(k, range(TIMES - k))
+            least = second.tile([P, TIMES - k], F32, tag="least")
             nc.vector.tensor_scalar(
                 out=least[:],
-                in0=minus_top[:, loss_cols(k)],
-                scalar1=math.log(P * n_s),
+                in0=minus_top[:, cols],
+                scalar1=math.log(P * (TIMES - k)),
                 scalar2=-1.0,
                 op0=ALU.add,
                 op1=ALU.mult,
             )
-            nc.vector.tensor_sub(out=offsets[:, loss_cols(k)], in0=least[:], in1=positive[:, loss_cols(k)])
+            for times, on_diagonal in zip(groups, products):
+                nc.vector.tensor_reduce(
+                    out=positive[:, loss_cols(k, times)], in_=on_diagonal[:], axis=AXIS.X, op=ALU.add
+                )
+            nc.vector.tensor_sub(out=offsets[:, cols], in0=least[:], in1=positive[:, cols])
+            place_values(placed_offsets, offsets, k)
+
+        def place_values(placed, values, k):
+            n_s = TIMES - k
+            cols = loss_cols(k, range(n_s))
+            nc.vector.tensor_tensor(
+                out=placed[:, cols.start * GATHER : cols.stop * GATHER].rearrange("p (l s) -> p l s", s=n_s),
+                in0=place[:].unsqueeze(2).to_broadcast([P, GATHER, n_s]),
+                in1=values[:, cols].unsqueeze(1).to_broadcast([P, GATHER, n_s]),
+                op=ALU.mult,
+            )
 
         def store_losses():
             logs = keep.tile([P, LOSSES], F32)
             nc.scalar.activation(out=logs[:], in_=exp_sums[:], func=ACT.Ln, scale=1.0)
-            loss = keep.tile([P, LOSSES], F32)
-            nc.vector.tensor_add(out=loss[:], in0=logs[:], in1=offsets[:])
-            placed = keep.tile([P, LOSSES * GATHER], F32)
+            placed_logs = keep.tile([P, LOSSES * GATHER], F32)
             for k in range(STEPS):
-                n_s = TIMES - k
-                first = loss_cols(k).start
-                nc.vector.tensor_tensor(
-                    out=placed[:, first * GATHER : (first + n_s) * GATHER].rearrange("p (l s) -> p l s", s=n_s),
-                    in0=place[:].unsqueeze(2).to_broadcast([P, GATHER, n_s]),
-                    in1=loss[:, loss_cols(k)].unsqueeze(1).to_broadcast([P, GATHER, n_s]),
-                    op=ALU.mult,
-                )
-            gathered = sums_psum.tile([P, LOSSES * GATHER], F32, tag=own_bank(0))
-            nc.tensor.matmul(out=gathered[:], lhsT=group[:], rhs=placed[:], start=True, stop=True)
+                place_values(placed_logs, logs, k)
+            gathered = sums_psum.tile([P, LOSSES * GATHER], F32, tag="sums2")
+            nc.tensor.matmul(out=gathered[:], lhsT=group[:], rhs=placed_offsets[:], start=True, stop=False)
+            nc.tensor.matmul(out=gathered[:], lhsT=group[:], rhs=placed_logs[:], start=False, stop=True)
             groups = P // GATHER
             runs = keep.tile([groups, LOSSES * GATHER], F32)
             nc.scalar.copy(out=runs[:], in_=gathered[0:groups, :])
             for k in range(STEPS):
                 n_s = TIMES - k
-                first = loss_cols(k).start
+                first = loss_cols(k, range(n_s)).start
                 queue = nc.scalar if k % 2 == 0 else nc.sync
                 queue.dma_start(
                     out=out[first * P : (first + n_s) * P].rearrange("(h n) -> h n", h=groups),
@@ -257,8 +274,8 @@ def tile_infonceloss_pa_k_kernel(tc, embeddings, contexts, W, out):
         x_scales = keep.tile([P, PASSES * ROWS], U8, align_bytes=64)
         sums = {}
 
-        def multiply(k, g, w_codes, w_scales):
-            for s in range(TIMES - k):
+        def multiply(k, g, w_codes, w_scales, times):
+            for s in times:
                 if g == 0:
                     sums[(k, s)] = sums_psum.tile([P, DY], F32, tag="sums%d" % s, name="sums_%d_%d" % (k, s))
                 cols = slice(g * ROWS + (k + s) * P, g * ROWS + (k + s + 1) * P)
@@ -324,20 +341,12 @@ def tile_infonceloss_pa_k_kernel(tc, embeddings, contexts, W, out):
         pieces = {}
 
         def plan_second(k, rnd):
-            if k < STEPS - 1:
-                halves = [range(first, min(first + 2, TIMES - k)) for first in range(0, TIMES - k, 2)]
-                todo = [[lambda: to_quantise.append(turn_xw(k, halves[0], own_bank(k), True))]]
-                todo += [[], [lambda: to_quantise.append(turn_xw(k, halves[1], own_bank(k), True))]]
-            else:
-                todo = [
-                    [
-                        lambda: to_quantise.append(turn_xw(k, [0], own_bank(0), True)),
-                        lambda: to_quantise.append(turn_xw(k, [1], own_bank(k), False)),
-                    ]
-                ]
-            todo += [[], [], [lambda: score(k)], [lambda: exponentials(k)], [lambda: diagonal(k)]]
-            if k == STEPS - 1:
-                todo += [[store_losses]]
+            times = range(TIMES - k)
+            bank = own_bank(k)
+            todo = [[lambda: to_quantise.append(turn_xw(k, times[0:2], bank))], []]
+            todo += [[lambda: to_quantise.append(turn_xw(k, times[2:], bank))]]
+            todo += [[], [], [lambda: score(k, times, bank)], [lambda: exponentials(k, times)]]
+            todo += [[lambda: diagonal(k, [times])]]
             for i, functions in enumerate(todo):
                 at = 2 * (rnd + 1) + 1 + i
                 pieces.setdefault((at // 2, at % 2), []).extend(functions)
@@ -348,7 +357,7 @@ def tile_infonceloss_pa_k_kernel(tc, embeddings, contexts, W, out):
 
         to_multiply = []
         quantised = {}
-        for rnd in range(len(rounds) + LAG + 4):
+        for rnd in range(len(rounds) + LAG):
             now_quantised = to_quantise
             to_quantise = []
             work_pieces(rnd, 0)
@@ -372,11 +381,32 @@ def tile_infonceloss_pa_k_kernel(tc, embeddings, contexts, W, out):
                 quantise(grouped, codes, scales)
             sort_ahead(starts[rnd + 2] + 1 if rnd + 2 < len(rounds) else len(turns))
             to_multiply += quantised.get(rnd - LAG, [])
-            while to_multiply:
+            while to_multiply and rnd < len(rounds) + LAG - 1:
                 k, g, w_codes, w_scales = to_multiply[0]
                 to_multiply = to_multiply[1:]
-                multiply(k, g, w_codes, w_scales)
+                times = range(TIMES - k)
+                multiply(k, g, w_codes, w_scales, times)
                 if g == PASSES - 1:
-                    round_xw(k)
+                    prepare_xw(k)
+                    for s in times:
+                        round_xw(k, s)
                     plan_second(k, rnd)
                     break
+
+        last = STEPS - 1
+        prepare_xw(last)
+        times = range(TIMES - last)
+        banks = [own_bank(0), own_bank(last)]
+        for s in times:
+            for k, g, w_codes, w_scales in to_multiply:
+                multiply(k, g, w_codes, w_scales, [s])
+            round_xw(last, s)
+        to_quantise = [turn_xw(last, [s], banks[s]) for s in times]
+        for grouped, codes, scales in to_quantise:
+            quantise(grouped, codes, scales)
+        for s in times:
+            score(last, [s], banks[s])
+        for s in times:
+            exponentials(last, [s])
+        diagonal(last, [[s] for s in times])
+        store_losses()

@@ -32,7 +32,6 @@ SINGLE = 6
 LAG = 2
 ALONE = 24
 CONTEXTS_ROUND = 14
-IDLE_PRODUCTS = 5
 LOSSES = 4 + 3 + 2
 GATHER = 8
 
@@ -55,12 +54,6 @@ def tile_infonceloss_pa_k_kernel(tc, embeddings, contexts, W, out):
         sums_psum = ctx.enter_context(tc.psum_pool(name="sums_psum", bufs=1))
         work_psum = ctx.enter_context(tc.psum_pool(name="work_psum", bufs=4))
         ctx.enter_context(tc.manual_schedule())
-
-        zeros = consts.tile([P, DY], BF16)
-        nc.vector.memset(zeros[:], 0.0)
-        for i in range(IDLE_PRODUCTS):
-            unused = work_psum.tile([P, DY], F32, tag="work", name="unused")
-            nc.tensor.matmul(out=unused[:], lhsT=zeros[:, 0:P], rhs=zeros[:], start=True, stop=True)
 
         ident_f32 = consts.tile([P, P], F32)
         make_identity(nc, ident_f32[:])

@@ -144,8 +144,6 @@ def tile_infonceloss_pa_k_kernel(tc, embeddings, contexts, W, out):
         exp_sums = keep.tile([P, LOSSES], F32)
         offsets = keep.tile([P, LOSSES], F32)
 
-        placed_offsets = keep.tile([P, LOSSES * GATHER], F32)
-
         def prepare_xw(k):
             xw_codes[k] = second.tile([P, TIMES * P], U32, tag="xw_codes", align_bytes=64, name="xw_codes_%d" % k)
             xw_scales[k] = second.tile([P, TIMES * P], U8, tag="xw_scales", align_bytes=64, name="xw_scales_%d" % k)
@@ -216,27 +214,24 @@ def tile_infonceloss_pa_k_kernel(tc, embeddings, contexts, W, out):
                     out=positive[:, loss_cols(k, times)], in_=on_diagonal[:], axis=AXIS.X, op=ALU.add
                 )
             nc.vector.tensor_sub(out=offsets[:, cols], in0=least[:], in1=positive[:, cols])
-            place_values(placed_offsets, offsets, k)
-
-        def place_values(placed, values, k):
-            n_s = TIMES - k
-            cols = loss_cols(k, range(n_s))
-            nc.vector.tensor_tensor(
-                out=placed[:, cols.start * GATHER : cols.stop * GATHER].rearrange("p (l s) -> p l s", s=n_s),
-                in0=place[:].unsqueeze(2).to_broadcast([P, GATHER, n_s]),
-                in1=values[:, cols].unsqueeze(1).to_broadcast([P, GATHER, n_s]),
-                op=ALU.mult,
-            )
 
         def store_losses():
             logs = keep.tile([P, LOSSES], F32)
             nc.scalar.activation(out=logs[:], in_=exp_sums[:], func=ACT.Ln, scale=1.0)
-            placed_logs = keep.tile([P, LOSSES * GATHER], F32)
+            loss = keep.tile([P, LOSSES], F32)
+            nc.vector.tensor_add(out=loss[:], in0=logs[:], in1=offsets[:])
+            placed = keep.tile([P, LOSSES * GATHER], F32)
             for k in range(STEPS):
-                place_values(placed_logs, logs, k)
-            gathered = sums_psum.tile([P, LOSSES * GATHER], F32, tag="sums2")
-            nc.tensor.matmul(out=gathered[:], lhsT=group[:], rhs=placed_offsets[:], start=True, stop=False)
-            nc.tensor.matmul(out=gathered[:], lhsT=group[:], rhs=placed_logs[:], start=False, stop=True)
+                n_s = TIMES - k
+                cols = loss_cols(k, range(n_s))
+                nc.vector.tensor_tensor(
+                    out=placed[:, cols.start * GATHER : cols.stop * GATHER].rearrange("p (l s) -> p l s", s=n_s),
+                    in0=place[:].unsqueeze(2).to_broadcast([P, GATHER, n_s]),
+                    in1=loss[:, cols].unsqueeze(1).to_broadcast([P, GATHER, n_s]),
+                    op=ALU.mult,
+                )
+            gathered = sums_psum.tile([P, LOSSES * GATHER], F32, tag=own_bank(0))
+            nc.tensor.matmul(out=gathered[:], lhsT=group[:], rhs=placed[:], start=True, stop=True)
             groups = P // GATHER
             runs = keep.tile([groups, LOSSES * GATHER], F32)
             nc.scalar.copy(out=runs[:], in_=gathered[0:groups, :])

import math
from contextlib import ExitStack

import concourse.mybir as mybir
from concourse.masks import make_identity

F32 = mybir.dt.float32
BF16 = mybir.dt.bfloat16
U32 = mybir.dt.uint32
U8 = mybir.dt.uint8
FP8X4 = mybir.dt.float8_e4m3fn_x4
ACT = mybir.ActivationFunctionType
ALU = mybir.AluOpType
AXIS = mybir.AxisListType

P = 128
DX = 8192
DY = 512
STEPS = 3
TIMES = 4
PACK = 4
K_PASS = P * PACK
PASSES = DX // K_PASS
BLOCKS = 4
ROWS = BLOCKS * P
LOAD_PASSES = 2
LOAD_D = LOAD_PASSES * K_PASS
PASS_WORDS = K_PASS // 2
HALF_BLOCK = 8
TURNS = 2
SINGLE = 6
LAG = 2
ALONE = 24
CONTEXTS_ROUND = 14
LOSSES = 4 + 3 + 2
GATHER = 8

FLOPS = 2 * (4 + 3 + 2) * P * DY * DX + 2 * (4 + 3 + 2) * P * P * DY
BYTES = 2 * (P * TIMES * DX + P * TIMES * DY + STEPS * DY * DX) + 4 * (4 + 3 + 2) * P


def tile_infonceloss_pa_k_kernel(tc, embeddings, contexts, W, out):
    nc = tc.nc
    with ExitStack() as ctx:
        consts = ctx.enter_context(tc.tile_pool(name="consts", bufs=1))
        keep = ctx.enter_context(tc.tile_pool(name="keep", bufs=1))
        loads = ctx.enter_context(tc.tile_pool(name="loads", bufs=7))
        sorted_loads = ctx.enter_context(tc.tile_pool(name="sorted_loads", bufs=4))
        stage = ctx.enter_context(tc.tile_pool(name="stage", bufs=2 * TURNS + 2))
        w_mx = ctx.enter_context(tc.tile_pool(name="w_mx", bufs=TURNS * (LAG + 2)))
        second = ctx.enter_context(tc.tile_pool(name="second", bufs=2))
        xw_rows = ctx.enter_context(tc.tile_pool(name="xw_rows", bufs=TIMES))
        e_stage = ctx.enter_context(tc.tile_pool(name="e_stage", bufs=2))
        sums_psum = ctx.enter_context(tc.psum_pool(name="sums_psum", bufs=1))
        work_psum = ctx.enter_context(tc.psum_pool(name="work_psum", bufs=4))
        ctx.enter_context(tc.manual_schedule())

        ident_f32 = consts.tile([P, P], F32)
        make_identity(nc, ident_f32[:])
        ident_bf16 = consts.tile([P, P], BF16)
        make_identity(nc, ident_bf16[:])
        group = consts.tile([P, P], F32)
        nc.vector.memset(group[:], 0.0)
        nc.vector.tensor_reduce(
            out=group[:, 0 : P // GATHER],
            in_=ident_f32[:].rearrange("p (h l) -> p h l", l=GATHER),
            axis=AXIS.X,
            op=ALU.add,
        )
        place = consts.tile([P, GATHER], F32)
        nc.vector.tensor_reduce(
            out=place[:], in_=ident_f32[:].rearrange("p (h l) -> p l h", l=GATHER), axis=AXIS.X, op=ALU.add
        )
        warm = consts.tile([P, 1], F32)
        nc.scalar.activation(out=warm[:], in_=place[:, 0:1], func=ACT.Exp)

        def load_rows(raw, rows_view, load):
            nc.sync.dma_start(
                out=raw[:].rearrange("p (r d) -> p r d", r=BLOCKS),
                in_=rows_view[:, :, load * LOAD_D : (load + 1) * LOAD_D],
            )

        def load_pass(raw, rows_view, g):
            i = g % LOAD_PASSES
            half = raw[:, i * BLOCKS * K_PASS : (i + 1) * BLOCKS * K_PASS]
            nc.sync.dma_start(
                out=half.rearrange("p (r d) -> p r d", r=BLOCKS),
                in_=rows_view[:, :, g * K_PASS : (g + 1) * K_PASS],
            )

        def sort_halves(halves, raw, cols):
            nc.vector.tensor_copy(
                out=halves[:, cols].rearrange("p (n u q i) -> p n u q i", u=2, q=K_PASS // 32, i=2 * HALF_BLOCK),
                in_=raw[:, cols].rearrange("p (n q u i) -> p n u q i", u=2, q=K_PASS // 32, i=2 * HALF_BLOCK),
            )

        def turn_pass(words):
            grouped = stage.tile([P, ROWS * PACK], BF16, tag="grouped", align_bytes=64)
            grouped_words = grouped[:].bitcast(F32).rearrange("p (c u) -> p c u", u=2)
            for half in range(2):
                bank = work_psum.tile([P, 2, 2 * P], F32, tag="work")
                for blk in range(2):
                    for u in range(2):
                        nc.tensor.transpose(
                            bank[:, u, blk * P : (blk + 1) * P], words[2 * half + blk][u], ident_f32[:]
                        )
                side_by_side = grouped_words[:, half * 2 * P : (half + 1) * 2 * P, :]
                nc.scalar.copy(out=side_by_side, in_=bank[:].rearrange("p u c -> p c u"))
            return grouped

        def sorted_words(halves, firsts):
            words = halves[:].bitcast(F32)
            return [[words[:, first + u * P : first + (u + 1) * P] for u in range(2)] for first in firsts]

        def quantise(grouped, codes, scales):
            nc.vector.quantize_mx(out=codes.bitcast(FP8X4), scales=scales, in_=grouped[:])

        def turn_xw(k, times, bank):
            n = len(times)
            cols = slice(times[0] * P, (times[-1] + 1) * P)
            turned = sums_psum.tile([P, n, PACK, P], BF16, tag=bank)
            for i in range(n):
                for t in range(PACK):
                    rows = xw[(k, times[i])][:, t * P : (t + 1) * P]
                    nc.tensor.transpose(turned[:, i, t, :], rows, ident_bf16[:])
            grouped = e_stage.tile([P, n * P * PACK], BF16, tag="grouped_e", align_bytes=64)
            side_by_side = grouped[:].rearrange("p (i r t) -> p i r t", i=n, t=PACK)
            nc.scalar.copy(out=side_by_side, in_=turned[:].rearrange("p i t r -> p i r t"))
            return (grouped, xw_codes[k][:, cols], xw_scales[k][:, cols])

        def own_bank(k):
            return "sums%d" % (TIMES - 1 - k)

        def loss_cols(k, times):
            first = sum(TIMES - j for j in range(k)) + times[0]
            return slice(first, first + len(times))

        xw = {}
        xw_codes = {}
        xw_scales = {}
        scores = {}
        minus_top = keep.tile([P, LOSSES], F32)
        positive = keep.tile([P, LOSSES], F32)
        exp_sums = keep.tile([P, LOSSES], F32)
        offsets = keep.tile([P, LOSSES], F32)

        def prepare_xw(k):
            xw_codes[k] = second.tile([P, TIMES * P], U32, tag="xw_codes", align_bytes=64, name="xw_codes_%d" % k)
            xw_scales[k] = second.tile([P, TIMES * P], U8, tag="xw_scales", align_bytes=64, name="xw_scales_%d" % k)

        def round_xw(k, s):
            xw[(k, s)] = xw_rows.tile([P, DY], BF16, tag="xw", name="xw_%d_%d" % (k, s))
            if s % 2 == 0:
                nc.scalar.copy(out=xw[(k, s)][:], in_=sums[(k, s)][:])
            else:
                nc.vector.tensor_copy(out=xw[(k, s)][:], in_=sums[(k, s)][:])

        def score(k, times, bank):
            n = len(times)
            found = sums_psum.tile([P, n, P], F32, tag=bank, name="scores_%d_%d" % (k, times[0]))
            scores[(k, times[0])] = found
            for i in range(n):
                cols = slice(times[i] * P, (times[i] + 1) * P)
                nc.tensor.matmul_mx(
                    out=found[:, i, :],
                    lhsT=xw_codes[k][:, cols].bitcast(FP8X4),
                    lhsT_scale=xw_scales[k][:, cols],
                    rhs=c_codes[:, cols].bitcast(FP8X4),
                    rhs_scale=c_scales[:, cols],
                    start=True,
                    stop=True,
                )
            nc.vector.tensor_reduce(
                out=minus_top[:, loss_cols(k, times)], in_=found[:], axis=AXIS.X, op=ALU.max, negate=True
            )

        def exponentials(k, times):
            exps = second.tile([P, len(times), P], F32, tag="exps")
            for i in range(len(times)):
                col = loss_cols(k, times[i : i + 1])
                nc.scalar.activation(
                    out=exps[:, i, :],
                    in_=scores[(k, times[0])][:, i, :],
                    func=ACT.Exp,
                    bias=minus_top[:, col],
                    scale=1.0,
                    accum_out=exp_sums[:, col],
                )

        def diagonal(k, groups):
            products = []
            for times in groups:
                n = len(times)
                on_diagonal = second.tile([P, n, P], F32, tag="on_diagonal")
                nc.vector.tensor_tensor(
                    out=on_diagonal[:],
                    in0=scores[(k, times[0])][:],
                    in1=ident_f32[:].unsqueeze(1).to_broadcast([P, n, P]),
                    op=ALU.mult,
                )
                products.append(on_diagonal)
            cols = loss_cols(k, range(TIMES - k))
            least = second.tile([P, TIMES - k], F32, tag="least")
            nc.vector.tensor_scalar(
                out=least[:],
                in0=minus_top[:, cols],
                scalar1=math.log(P * (TIMES - k)),
                scalar2=-1.0,
                op0=ALU.add,
                op1=ALU.mult,
            )
            for times, on_diagonal in zip(groups, products):
                nc.vector.tensor_reduce(
                    out=positive[:, loss_cols(k, times)], in_=on_diagonal[:], axis=AXIS.X, op=ALU.add
                )
            nc.vector.tensor_sub(out=offsets[:, cols], in0=least[:], in1=positive[:, cols])

        def store_losses():
            logs = keep.tile([P, LOSSES], F32)
            nc.scalar.activation(out=logs[:], in_=exp_sums[:], func=ACT.Ln, scale=1.0)
            loss = keep.tile([P, LOSSES], F32)
            nc.vector.tensor_add(out=loss[:], in0=logs[:], in1=offsets[:])
            placed = keep.tile([P, LOSSES * GATHER], F32)
            for k in range(STEPS):
                n_s = TIMES - k
                cols = loss_cols(k, range(n_s))
                nc.vector.tensor_tensor(
                    out=placed[:, cols.start * GATHER : cols.stop * GATHER].rearrange("p (l s) -> p l s", s=n_s),
                    in0=place[:].unsqueeze(2).to_broadcast([P, GATHER, n_s]),
                    in1=loss[:, cols].unsqueeze(1).to_broadcast([P, GATHER, n_s]),
                    op=ALU.mult,
                )
            gathered = sums_psum.tile([P, LOSSES * GATHER], F32, tag=own_bank(0))
            nc.tensor.matmul(out=gathered[:], lhsT=group[:], rhs=placed[:], start=True, stop=True)
            groups = P // GATHER
            runs = keep.tile([groups, LOSSES * GATHER], F32)
            nc.scalar.copy(out=runs[:], in_=gathered[0:groups, :])
            for k in range(STEPS):
                n_s = TIMES - k
                first = loss_cols(k, range(n_s)).start
                queue = nc.scalar if k % 2 == 0 else nc.sync
                queue.dma_start(
                    out=out[first * P : (first + n_s) * P].rearrange("(h n) -> h n", h=groups),
                    in_=runs[:, first * GATHER : (first + n_s) * GATHER],
                )

        c_codes = keep.tile([P, TIMES * P], U32, align_bytes=64)
        c_scales = keep.tile([P, TIMES * P], U8, align_bytes=64)

        def load_contexts():
            c_raw = keep.tile([P, TIMES * DY], BF16, name="c_raw")
            nc.sync.dma_start(out=c_raw[:].rearrange("p (t e) -> p t e", t=TIMES), in_=contexts[:, 0:TIMES, :])
            return c_raw

        def turn_contexts(c_raw):
            words = c_raw[:].bitcast(F32).rearrange("b (t p u) -> b t u p", t=TIMES, u=2)
            turned = turn_pass([[words[:, t, u, :] for u in range(2)] for t in range(TIMES)])
            return (turned, c_codes[:], c_scales[:])

        x_view = embeddings[:, 1 : 1 + TIMES, :]
        x_codes = keep.tile([P, PASSES * ROWS], U32, align_bytes=64)
        x_scales = keep.tile([P, PASSES * ROWS], U8, align_bytes=64)
        sums = {}

        def multiply(k, g, w_codes, w_scales, times):
            for s in times:
                if g == 0:
                    sums[(k, s)] = sums_psum.tile([P, DY], F32, tag="sums%d" % s, name="sums_%d_%d" % (k, s))
                cols = slice(g * ROWS + (k + s) * P, g * ROWS + (k + s + 1) * P)
                nc.tensor.matmul_mx(
                    out=sums[(k, s)][:],
                    lhsT=x_codes[:, cols].bitcast(FP8X4),
                    lhsT_scale=x_scales[:, cols],
                    rhs=w_codes[:].bitcast(FP8X4),
                    rhs_scale=w_scales[:],
                    start=(g == 0),
                    stop=(g == PASSES - 1),
                )

        turns = []
        for k in range(STEPS):
            for g in range(PASSES):
                if k == 0:
                    turns.append((None, g))
                turns.append((k, g))
        starts = list(range(SINGLE)) + list(range(SINGLE, len(turns), TURNS))
        rounds = [turns[first:after] for first, after in zip(starts, starts[1:] + [len(turns)])]

        def view(k):
            return x_view if k is None else W[k].rearrange("(p r) d -> p r d", r=BLOCKS)

        halves_of = {}
        firsts_of = {}

        raws = {}

        def load(k, g):
            key = (k, g // LOAD_PASSES)
            alone = turns.index((k, g)) < ALONE
            if key not in raws:
                raws[key] = loads.tile([P, BLOCKS * LOAD_D], BF16, tag="raw", name="raw_%s_%d" % key)
                halves_of[key] = sorted_loads.tile([P, BLOCKS * LOAD_D], BF16, tag="halves", name="halves_%s_%d" % key)
                if not alone:
                    load_rows(raws[key], view(k), key[1])
            if alone:
                load_pass(raws[key], view(k), g)
            return alone

        def load_and_sort(k, g):
            key = (k, g // LOAD_PASSES)
            i = g % LOAD_PASSES
            if load(k, g):
                cols = slice(i * BLOCKS * K_PASS, (i + 1) * BLOCKS * K_PASS)
                firsts_of[(k, g)] = [(i * BLOCKS + r) * PASS_WORDS for r in range(BLOCKS)]
            else:
                cols = slice(0, BLOCKS * LOAD_D)
                for j in range(LOAD_PASSES):
                    firsts_of[(k, g - i + j)] = [(r * LOAD_PASSES + j) * PASS_WORDS for r in range(BLOCKS)]
            sort_halves(halves_of[key], raws[key], cols)

        def sort_ahead(n):
            for k, g in turns[:n]:
                if (k, g) not in firsts_of:
                    load_and_sort(k, g)

        sort_ahead(starts[1] + 1)

        to_quantise = []
        pieces = {}

        def plan_second(k, rnd):
            times = range(TIMES - k)
            bank = own_bank(k)
            todo = [[lambda: to_quantise.append(turn_xw(k, times[0:2], bank))], []]
            todo += [[lambda: to_quantise.append(turn_xw(k, times[2:], bank))]]
            todo += [[], [], [lambda: score(k, times, bank)], [lambda: exponentials(k, times)]]
            todo += [[lambda: diagonal(k, [times])]]
            for i, functions in enumerate(todo):
                at = 2 * (rnd + 1) + 1 + i
                pieces.setdefault((at // 2, at % 2), []).extend(functions)

        def work_pieces(rnd, place):
            for piece in pieces.get((rnd, place), []):
                piece()

        to_multiply = []
        quantised = {}
        for rnd in range(len(rounds) + LAG):
            now_quantised = to_quantise
            to_quantise = []
            work_pieces(rnd, 0)
            quantised[rnd] = []
            for k, g in rounds[rnd] if rnd < len(rounds) else []:
                grouped = turn_pass(sorted_words(halves_of[(k, g // LOAD_PASSES)], firsts_of[(k, g)]))
                if k is None:
                    cols = slice(g * ROWS, (g + 1) * ROWS)
                    to_quantise.append((grouped, x_codes[:, cols], x_scales[:, cols]))
                else:
                    w_codes = w_mx.tile([P, ROWS], U32, tag="w_codes", align_bytes=64)
                    w_scales = w_mx.tile([P, ROWS], U8, tag="w_scales", align_bytes=64)
                    to_quantise.append((grouped, w_codes[:], w_scales[:]))
                    quantised[rnd].append((k, g, w_codes, w_scales))
            if rnd == CONTEXTS_ROUND - 2:
                c_raw = load_contexts()
            if rnd == CONTEXTS_ROUND:
                to_quantise.append(turn_contexts(c_raw))
            work_pieces(rnd, 1)
            for grouped, codes, scales in now_quantised:
                quantise(grouped, codes, scales)
            sort_ahead(starts[rnd + 2] + 1 if rnd + 2 < len(rounds) else len(turns))
            to_multiply += quantised.get(rnd - LAG, [])
            while to_multiply and rnd < len(rounds) + LAG - 1:
                k, g, w_codes, w_scales = to_multiply[0]
                to_multiply = to_multiply[1:]
                times = range(TIMES - k)
                multiply(k, g, w_codes, w_scales, times)
                if g == PASSES - 1:
                    prepare_xw(k)
                    for s in times:
                        round_xw(k, s)
                    plan_second(k, rnd)
                    break

        last = STEPS - 1
        prepare_xw(last)
        times = range(TIMES - last)
        banks = [own_bank(0), own_bank(last)]
        for s in times:
            for k, g, w_codes, w_scales in to_multiply:
                multiply(k, g, w_codes, w_scales, [s])
            round_xw(last, s)
        to_quantise = [turn_xw(last, [s], banks[s]) for s in times]
        for grouped, codes, scales in to_quantise:
            quantise(grouped, codes, scales)
        for s in times:
            score(last, [s], banks[s])
        for s in times:
            exponentials(last, [s])
        diagonal(last, [[s] for s in times])
        store_losses()
